import numpy as np
import ml_dtypes


def mxq(x, axis, fmt="e4m3"):
    dtype, down = {"e4m3": (ml_dtypes.float8_e4m3fn, 7), "e5m2": (ml_dtypes.float8_e5m2, 14)}[fmt]
    v = np.moveaxis(np.asarray(x, np.float32).astype(ml_dtypes.bfloat16).astype(np.float64), axis, -1)
    blocks = v.reshape(v.shape[:-1] + (-1, 32))
    amax = np.abs(blocks).max(-1, keepdims=True)
    byte = np.maximum(np.where(amax > 0, np.frexp(amax)[1] - 1 + 127, 0) - down, 1)
    scale = np.exp2(byte - 127.0)
    codes = (blocks / scale).astype(np.float32).astype(dtype).astype(np.float64)
    return np.moveaxis((codes * scale).reshape(v.shape), -1, axis)


WIDE = False


def mx_kscale(k):
    if not WIDE:
        return np.ones(k)
    levels = np.array([10, -10, 5, -5, 0])
    a = np.random.permutation(np.resize(levels, k // 512 * 4)).reshape(k // 512, 4)
    idx = np.arange(k)
    return np.exp2(a[idx // 512, idx % 128 // 32])


BF16 = ml_dtypes.bfloat16


def bf(x):
    return np.asarray(x, np.float32).astype(BF16)


def f64(x):
    return np.asarray(x).astype(np.float64)


B, CI, C, VI, V, N, M = 3, 1024, 128, 512, 512, 4096, 1024
EPS = 1e-5
QS = np.sqrt(2.0) / C ** 0.25


def instance_norm(x):
    mu = x.mean(-1, keepdims=True)
    var = np.square(x - mu).mean(-1, keepdims=True)
    return (x - mu) * (1.0 / np.sqrt(var + EPS))


def norm_rms(a):
    return a / np.sqrt(a * a + EPS)


def setup_inputs():
    k = mx_kscale(CI)
    t = (k / k.max())[:, None]
    g = np.exp2(np.random.uniform(-8.0, 1.0, (CI, 1)))
    d = np.exp2(np.round(np.log2(norm_rms(g * t) / norm_rms(g))))[:, 0]
    q = g * t * (np.random.standard_normal((B, CI, N)) + 0.5 * np.random.standard_normal((B, CI, 1)))
    return {"q": bf(q), "Wq": bf(np.random.standard_normal((C, CI)) * QS / np.sqrt(CI) / d[None, :]), "bq": bf(np.random.standard_normal(C) * 0.3 * QS)}


def reference(q, Wq, bq):
    xn = instance_norm(f64(q))
    return (mxq(f64(Wq), 1, "e4m3") @ mxq(xn, 1, "e4m3")) + f64(bq)[None, :, None]

@@ -1,0 +1,196 @@
+from contextlib import ExitStack
+
+import concourse.mybir as mybir
+from concourse.masks import make_identity
+
+FLOPS = 2 * 3 * 128 * 1024 * 4096
+
+F32 = mybir.dt.float32
+BF16 = mybir.dt.bfloat16
+U32 = mybir.dt.uint32
+U8 = mybir.dt.uint8
+FP8X4 = mybir.dt.float8_e4m3fn_x4
+ALU = mybir.AluOpType
+ACT = mybir.ActivationFunctionType
+
+EPS = 1e-5
+P = 128
+PACK = 4
+K_PASS = P * PACK
+BANK = 512
+CHUNK = 1024
+RUN = 4
+RAW_BUFS = 4
+MEANS_AHEAD = RAW_BUFS - 1
+
+
+def tile_adaattn3dstylizer_pa_t_kernel(tc, q, Wq, bq, out):
+    nc = tc.nc
+    batches, channels, positions = q.shape
+    passes = channels // K_PASS
+    tiles = batches * passes
+    chunks = positions // CHUNK
+    assert Wq.shape[0] == P and channels % K_PASS == 0 and positions % CHUNK == 0
+    assert chunks == PACK
+
+    with ExitStack() as ctx:
+        const = ctx.enter_context(tc.tile_pool(name="const", bufs=1))
+        raw_pool = ctx.enter_context(tc.tile_pool(name="raw", bufs=RAW_BUFS))
+        stat_pool = ctx.enter_context(tc.tile_pool(name="stat", bufs=tiles))
+        scrap_pool = ctx.enter_context(tc.tile_pool(name="scrap", bufs=2))
+        group_pool = ctx.enter_context(tc.tile_pool(name="group", bufs=chunks))
+        code_pool = ctx.enter_context(tc.tile_pool(name="code", bufs=3))
+        out_pool = ctx.enter_context(tc.tile_pool(name="outs", bufs=2))
+        ctx.enter_context(tc.manual_schedule())
+
+        x = {}
+        neg_mean, sum_sq, rstd = {}, {}, {}
+        acc = {}
+
+        def load(i):
+            b, g = divmod(i, passes)
+            rows = q[b, g * K_PASS : (g + 1) * K_PASS, :].rearrange("(p t) n -> p t n", t=PACK)
+            x[i] = raw_pool.tile([P, PACK, positions], BF16, name="x")
+            for t in range(PACK):
+                nc.sync.dma_start(out=x[i][:, t, :], in_=rows[:, t, :])
+
+        def statistics_row(i, t):
+            if t == 0:
+                neg_mean[i] = stat_pool.tile([P, PACK], F32, name="neg_mean")
+                sum_sq[i] = stat_pool.tile([P, PACK], F32, name="sum_sq")
+            scrap_v = scrap_pool.tile([P, positions], BF16, name="scrap_v")
+            nc.vector.tensor_scalar(
+                out=scrap_v[:],
+                in0=x[i][:, t, :],
+                scalar1=-1.0 / positions,
+                scalar2=None,
+                op0=ALU.mult,
+                op1=ALU.add,
+                accum_out=neg_mean[i][:, t : t + 1],
+            )
+            scrap_s = scrap_pool.tile([P, positions], BF16, name="scrap_s")
+            nc.scalar.activation(
+                out=scrap_s[:],
+                in_=x[i][:, t, :],
+                func=ACT.Square,
+                bias=neg_mean[i][:, t : t + 1],
+                scale=1.0,
+                accum_out=sum_sq[i][:, t : t + 1],
+            )
+
+        def finish_statistics(i):
+            var_eps = stat_pool.tile([P, PACK], F32, name="var_eps")
+            nc.vector.tensor_scalar(
+                out=var_eps[:], in0=sum_sq[i][:], scalar1=1.0 / positions, scalar2=EPS, op0=ALU.mult, op1=ALU.add
+            )
+            rstd[i] = stat_pool.tile([P, PACK], F32, name="rstd")
+            nc.gpsimd.tensor_tensor(out=rstd[i][:], in0=var_eps[:], in1=minus_half[:], op=ALU.pow)
+
+        def normalise(i):
+            for t in range(PACK):
+                nc.vector.tensor_scalar(
+                    out=x[i][:, t, :],
+                    in0=x[i][:, t, :],
+                    scalar1=neg_mean[i][:, t : t + 1],
+                    scalar2=rstd[i][:, t : t + 1],
+                    op0=ALU.add,
+                    op1=ALU.mult,
+                )
+
+        def regroup(i, c, on_scalar):
+            grouped = group_pool.tile([P, CHUNK, PACK], BF16, align_bytes=64, name="grouped")
+            src = x[i][:, :, c * CHUNK : (c + 1) * CHUNK].rearrange("p t (r s) -> p r t s", s=RUN)
+            dst = grouped[:].rearrange("p (r s) t -> p r t s", s=RUN)
+            if on_scalar:
+                nc.scalar.copy(out=dst, in_=src)
+            else:
+                nc.vector.tensor_copy(out=dst, in_=src)
+            return grouped
+
+        def quantise_and_project(i, c, grouped):
+            b, g = divmod(i, passes)
+            codes = code_pool.tile([P, CHUNK], U32, align_bytes=64, name="codes")
+            scales = code_pool.tile([P, CHUNK], U8, align_bytes=64, name="scales")
+            nc.vector.quantize_mx(
+                out=codes[:].bitcast(FP8X4), scales=scales[:], in_=grouped[:].rearrange("p n t -> p (n t)")
+            )
+            for h in range(CHUNK // BANK):
+                cols = slice(h * BANK, (h + 1) * BANK)
+                if g == 0:
+                    acc[c, h] = psum.tile([P, BANK], F32, name="acc")
+                nc.tensor.matmul_mx(
+                    out=acc[c, h][:],
+                    lhsT=w_codes[:, g, :].bitcast(FP8X4),
+                    lhsT_scale=w_scales[:, g, :],
+                    rhs=codes[:, cols].bitcast(FP8X4),
+                    rhs_scale=scales[:, cols],
+                    start=(g == 0),
+                    stop=(g == passes - 1),
+                )
+            if g == passes - 1:
+                result = out_pool.tile([P, CHUNK], F32, name="result")
+                for h in range(CHUNK // BANK):
+                    nc.scalar.activation(
+                        out=result[:, h * BANK : (h + 1) * BANK],
+                        in_=acc[c, h][:],
+                        func=ACT.Identity,
+                        bias=bias[:, 0:1],
+                        scale=1.0,
+                    )
+                nc.scalar.dma_start(out=out[b, :, c * CHUNK : (c + 1) * CHUNK], in_=result[:])
+
+        w_rows = const.tile([P, channels], BF16)
+        nc.scalar.dma_start(out=w_rows[:], in_=Wq)
+        for i in range(min(RAW_BUFS, tiles)):
+            load(i)
+        identity = const.tile([P, P], BF16)
+        make_identity(nc, identity[:])
+        minus_half = const.tile([P, PACK], F32)
+        nc.vector.memset(minus_half[:], -0.5)
+        bias_rows = const.tile([P, P], BF16)
+        nc.vector.memset(bias_rows[:], 0.0)
+        nc.scalar.dma_start(out=bias_rows[0:1, :], in_=bq.rearrange("(x o) -> x o", x=1))
+        warm = const.tile([P, PACK], F32)
+        nc.scalar.activation(out=warm[:], in_=minus_half[:], func=ACT.Square)
+
+        w_sorted = const.tile([P, passes, PACK, P], BF16)
+        nc.vector.tensor_copy(out=w_sorted[:], in_=w_rows[:].rearrange("o (g p t) -> o g t p", g=passes, t=PACK))
+        w_grouped = const.tile([P, passes, P, PACK], BF16, align_bytes=64)
+        bias = const.tile([P, 1], F32)
+        with tc.psum_pool(name="setup", bufs=1) as setup:
+            w_turned = setup.tile([P, passes, PACK, P], BF16)
+            for g in range(passes):
+                for t in range(PACK):
+                    nc.tensor.transpose(w_turned[:, g, t, :], w_sorted[:, g, t, :], identity[:])
+            bias_turned = setup.tile([P, P], BF16)
+            nc.tensor.transpose(bias_turned[:], bias_rows[:], identity[:])
+            nc.scalar.copy(out=w_grouped[:], in_=w_turned[:].rearrange("p g t o -> p g o t"))
+            nc.scalar.copy(out=bias[:], in_=bias_turned[:, 0:1])
+        psum = ctx.enter_context(tc.psum_pool(name="psum", bufs=8))
+
+        for i in range(min(MEANS_AHEAD, tiles)):
+            for t in range(PACK):
+                statistics_row(i, t)
+        finish_statistics(0)
+        w_codes = const.tile([P, passes, P], U32, align_bytes=64)
+        w_scales = const.tile([P, passes, P], U8, align_bytes=64)
+        nc.vector.quantize_mx(
+            out=w_codes[:].rearrange("p g o -> p (g o)").bitcast(FP8X4),
+            scales=w_scales[:].rearrange("p g o -> p (g o)"),
+            in_=w_grouped[:].rearrange("p g o t -> p (g o t)"),
+        )
+
+        for i in range(tiles):
+            later = i + MEANS_AHEAD
+            normalise(i)
+            grouped = []
+            for c in range(chunks):
+                grouped.append(regroup(i, c, on_scalar=(later >= tiles and c % 2 == 1)))
+                if later < tiles:
+                    statistics_row(later, c)
+            if i + RAW_BUFS < tiles:
+                load(i + RAW_BUFS)
+            if i + 1 < tiles:
+                finish_statistics(i + 1)
+            for c in range(chunks):
+                quantise_and_project(i, c, grouped[c])

@@ -32,6 +32,7 @@ def tile_adaattn3dstylizer_pa_t_kernel(tc, q, Wq, bq, out):
     chunks = positions // CHUNK
     assert Wq.shape[0] == P and channels % K_PASS == 0 and positions % CHUNK == 0
     assert chunks == PACK
+    assert tiles >= RAW_BUFS
 
     with ExitStack() as ctx:
         const = ctx.enter_context(tc.tile_pool(name="const", bufs=1))
@@ -40,7 +41,7 @@ def tile_adaattn3dstylizer_pa_t_kernel(tc, q, Wq, bq, out):
         scrap_pool = ctx.enter_context(tc.tile_pool(name="scrap", bufs=2))
         group_pool = ctx.enter_context(tc.tile_pool(name="group", bufs=chunks))
         code_pool = ctx.enter_context(tc.tile_pool(name="code", bufs=3))
-        out_pool = ctx.enter_context(tc.tile_pool(name="outs", bufs=2))
+        out_pool = ctx.enter_context(tc.tile_pool(name="outs", bufs=4))
         ctx.enter_context(tc.manual_schedule())
 
         x = {}
@@ -137,11 +138,11 @@ def tile_adaattn3dstylizer_pa_t_kernel(tc, q, Wq, bq, out):
                         bias=bias[:, 0:1],
                         scale=1.0,
                     )
-                nc.scalar.dma_start(out=out[b, :, c * CHUNK : (c + 1) * CHUNK], in_=result[:])
+                nc.sync.dma_start(out=out[b, :, c * CHUNK : (c + 1) * CHUNK], in_=result[:])
 
         w_rows = const.tile([P, channels], BF16)
         nc.scalar.dma_start(out=w_rows[:], in_=Wq)
-        for i in range(min(RAW_BUFS, tiles)):
+        for i in range(RAW_BUFS):
             load(i)
         identity = const.tile([P, P], BF16)
         make_identity(nc, identity[:])
@@ -168,10 +169,11 @@ def tile_adaattn3dstylizer_pa_t_kernel(tc, q, Wq, bq, out):
             nc.scalar.copy(out=bias[:], in_=bias_turned[:, 0:1])
         psum = ctx.enter_context(tc.psum_pool(name="psum", bufs=8))
 
-        for i in range(min(MEANS_AHEAD, tiles)):
+        for i in range(MEANS_AHEAD):
             for t in range(PACK):
+                if i == MEANS_AHEAD - 1 and t == PACK // 2:
+                    finish_statistics(0)
                 statistics_row(i, t)
-        finish_statistics(0)
         w_codes = const.tile([P, passes, P], U32, align_bytes=64)
         w_scales = const.tile([P, passes, P], U8, align_bytes=64)
         nc.vector.quantize_mx(
@@ -180,17 +182,20 @@ def tile_adaattn3dstylizer_pa_t_kernel(tc, q, Wq, bq, out):
             in_=w_grouped[:].rearrange("p g o t -> p (g o t)"),
         )
 
+        normalise(0)
+
         for i in range(tiles):
             later = i + MEANS_AHEAD
-            normalise(i)
             grouped = []
             for c in range(chunks):
+                if c == chunks // 2 and i + 1 < tiles:
+                    finish_statistics(i + 1)
                 grouped.append(regroup(i, c, on_scalar=(later >= tiles and c % 2 == 1)))
                 if later < tiles:
                     statistics_row(later, c)
             if i + RAW_BUFS < tiles:
                 load(i + RAW_BUFS)
             if i + 1 < tiles:
-                finish_statistics(i + 1)
+                normalise(i + 1)
             for c in range(chunks):
                 quantise_and_project(i, c, grouped[c])

@@ -98,14 +98,24 @@ def tile_adaattn3dstylizer_pa_t_kernel(tc, q, Wq, bq, out):
                     op1=ALU.mult,
                 )
 
-        def regroup(i, c, on_scalar):
+        def regroup(i, c, engine):
             grouped = group_pool.tile([P, CHUNK, PACK], BF16, align_bytes=64, name="grouped")
-            src = x[i][:, :, c * CHUNK : (c + 1) * CHUNK].rearrange("p t (r s) -> p r t s", s=RUN)
+            cols = x[i][:, :, c * CHUNK : (c + 1) * CHUNK]
+            src = cols.rearrange("p t (r s) -> p r t s", s=RUN)
             dst = grouped[:].rearrange("p (r s) t -> p r t s", s=RUN)
-            if on_scalar:
+            if engine == "vector":
+                nc.vector.tensor_copy(out=dst, in_=src)
+            elif engine == "scalar":
                 nc.scalar.copy(out=dst, in_=src)
             else:
-                nc.vector.tensor_copy(out=dst, in_=src)
+                nc.gpsimd.tensor_scalar(
+                    out=grouped[:],
+                    in0=cols.rearrange("p t n -> p n t"),
+                    scalar1=1.0,
+                    scalar2=0.0,
+                    op0=ALU.mult,
+                    op1=ALU.add,
+                )
             return grouped
 
         def quantise_and_project(i, c, grouped):
@@ -186,13 +196,16 @@ def tile_adaattn3dstylizer_pa_t_kernel(tc, q, Wq, bq, out):
 
         for i in range(tiles):
             later = i + MEANS_AHEAD
-            grouped = []
+            grouped = {}
+            if later < tiles:
+                grouped[chunks - 1] = regroup(i, chunks - 1, "gpsimd")
+                for t in range(PACK):
+                    statistics_row(later, t)
+            if i + 1 < tiles:
+                finish_statistics(i + 1)
             for c in range(chunks):
-                if c == chunks // 2 and i + 1 < tiles:
-                    finish_statistics(i + 1)
-                grouped.append(regroup(i, c, on_scalar=(later >= tiles and c % 2 == 1)))
-                if later < tiles:
-                    statistics_row(later, c)
+                if c not in grouped:
+                    grouped[c] = regroup(i, c, "scalar" if later >= tiles and c % 2 == 1 else "vector")
             if i + RAW_BUFS < tiles:
                 load(i + RAW_BUFS)
             if i + 1 < tiles:

@@ -41,7 +41,7 @@ def tile_adaattn3dstylizer_pa_t_kernel(tc, q, Wq, bq, out):
         scrap_pool = ctx.enter_context(tc.tile_pool(name="scrap", bufs=2))
         group_pool = ctx.enter_context(tc.tile_pool(name="group", bufs=chunks))
         code_pool = ctx.enter_context(tc.tile_pool(name="code", bufs=3))
-        out_pool = ctx.enter_context(tc.tile_pool(name="outs", bufs=4))
+        out_pool = ctx.enter_context(tc.tile_pool(name="outs", bufs=8))
         ctx.enter_context(tc.manual_schedule())
 
         x = {}
@@ -139,16 +139,13 @@ def tile_adaattn3dstylizer_pa_t_kernel(tc, q, Wq, bq, out):
                     stop=(g == passes - 1),
                 )
             if g == passes - 1:
-                result = out_pool.tile([P, CHUNK], F32, name="result")
                 for h in range(CHUNK // BANK):
+                    first = c * CHUNK + h * BANK
+                    result = out_pool.tile([P, BANK], F32, name="result")
                     nc.scalar.activation(
-                        out=result[:, h * BANK : (h + 1) * BANK],
-                        in_=acc[c, h][:],
-                        func=ACT.Identity,
-                        bias=bias[:, 0:1],
-                        scale=1.0,
+                        out=result[:], in_=acc[c, h][:], func=ACT.Identity, bias=bias[:, 0:1], scale=1.0
                     )
-                nc.sync.dma_start(out=out[b, :, c * CHUNK : (c + 1) * CHUNK], in_=result[:])
+                    nc.sync.dma_start(out=out[b, :, first : first + BANK], in_=result[:])
 
         w_rows = const.tile([P, channels], BF16)
         nc.scalar.dma_start(out=w_rows[:], in_=Wq)
@@ -166,6 +163,9 @@ def tile_adaattn3dstylizer_pa_t_kernel(tc, q, Wq, bq, out):
 
         w_sorted = const.tile([P, passes, PACK, P], BF16)
         nc.vector.tensor_copy(out=w_sorted[:], in_=w_rows[:].rearrange("o (g p t) -> o g t p", g=passes, t=PACK))
+
+        for t in range(PACK):
+            statistics_row(0, t)
         w_grouped = const.tile([P, passes, P, PACK], BF16, align_bytes=64)
         bias = const.tile([P, 1], F32)
         with tc.psum_pool(name="setup", bufs=1) as setup:
@@ -179,7 +179,7 @@ def tile_adaattn3dstylizer_pa_t_kernel(tc, q, Wq, bq, out):
             nc.scalar.copy(out=bias[:], in_=bias_turned[:, 0:1])
         psum = ctx.enter_context(tc.psum_pool(name="psum", bufs=8))
 
-        for i in range(MEANS_AHEAD):
+        for i in range(1, MEANS_AHEAD):
             for t in range(PACK):
                 if i == MEANS_AHEAD - 1 and t == PACK // 2:
                     finish_statistics(0)

@@ -45,7 +45,7 @@ def tile_adaattn3dstylizer_pa_t_kernel(tc, q, Wq, bq, out):
         ctx.enter_context(tc.manual_schedule())
 
         x = {}
-        neg_mean, sum_sq, rstd = {}, {}, {}
+        neg_mean, sum_sq, std, rstd = {}, {}, {}, {}
         acc = {}
 
         def load(i):
@@ -78,14 +78,13 @@ def tile_adaattn3dstylizer_pa_t_kernel(tc, q, Wq, bq, out):
                 scale=1.0,
                 accum_out=sum_sq[i][:, t : t + 1],
             )
+            if t == PACK - 1:
+                std[i] = stat_pool.tile([P, PACK], F32, name="std")
+                nc.scalar.activation(out=std[i][:], in_=sum_sq[i][:], func=ACT.Sqrt, bias=EPS, scale=1.0 / positions)
 
         def finish_statistics(i):
-            var_eps = stat_pool.tile([P, PACK], F32, name="var_eps")
-            nc.vector.tensor_scalar(
-                out=var_eps[:], in0=sum_sq[i][:], scalar1=1.0 / positions, scalar2=EPS, op0=ALU.mult, op1=ALU.add
-            )
             rstd[i] = stat_pool.tile([P, PACK], F32, name="rstd")
-            nc.gpsimd.tensor_tensor(out=rstd[i][:], in0=var_eps[:], in1=minus_half[:], op=ALU.pow)
+            nc.vector.reciprocal(out=rstd[i][:], in_=std[i][:])
 
         def normalise(i):
             for t in range(PACK):
@@ -153,13 +152,13 @@ def tile_adaattn3dstylizer_pa_t_kernel(tc, q, Wq, bq, out):
             load(i)
         identity = const.tile([P, P], BF16)
         make_identity(nc, identity[:])
-        minus_half = const.tile([P, PACK], F32)
-        nc.vector.memset(minus_half[:], -0.5)
+        ones = const.tile([P, PACK], F32)
+        nc.vector.memset(ones[:], 1.0)
         bias_rows = const.tile([P, P], BF16)
         nc.vector.memset(bias_rows[:], 0.0)
         nc.scalar.dma_start(out=bias_rows[0:1, :], in_=bq.rearrange("(x o) -> x o", x=1))
         warm = const.tile([P, PACK], F32)
-        nc.scalar.activation(out=warm[:], in_=minus_half[:], func=ACT.Square)
+        nc.scalar.activation(out=warm[:], in_=ones[:], func=ACT.Sqrt)
 
         w_sorted = const.tile([P, passes, PACK, P], BF16)
         nc.vector.tensor_copy(out=w_sorted[:], in_=w_rows[:].rearrange("o (g p t) -> o g t p", g=passes, t=PACK))

@@ -20,8 +20,9 @@ K_PASS = P * PACK
 BANK = 512
 CHUNK = 1024
 RUN = 4
+PIECE = 512
 RAW_BUFS = 4
-MEANS_AHEAD = RAW_BUFS - 1
+AHEAD = 2
 
 
 def tile_adaattn3dstylizer_pa_t_kernel(tc, q, Wq, bq, out):
@@ -31,7 +32,7 @@ def tile_adaattn3dstylizer_pa_t_kernel(tc, q, Wq, bq, out):
     tiles = batches * passes
     chunks = positions // CHUNK
     assert Wq.shape[0] == P and channels % K_PASS == 0 and positions % CHUNK == 0
-    assert chunks == PACK
+    assert chunks % 2 == 0 and CHUNK == 2 * PIECE
     assert tiles >= RAW_BUFS
 
     with ExitStack() as ctx:
@@ -97,25 +98,25 @@ def tile_adaattn3dstylizer_pa_t_kernel(tc, q, Wq, bq, out):
                     op1=ALU.mult,
                 )
 
-        def regroup(i, c, engine):
-            grouped = group_pool.tile([P, CHUNK, PACK], BF16, align_bytes=64, name="grouped")
-            cols = x[i][:, :, c * CHUNK : (c + 1) * CHUNK]
+        def regroup(i, grouped, first, count, engine):
+            c, start = divmod(first, CHUNK)
+            target = grouped[c][:, start : start + count, :]
+            cols = x[i][:, :, first : first + count]
             src = cols.rearrange("p t (r s) -> p r t s", s=RUN)
-            dst = grouped[:].rearrange("p (r s) t -> p r t s", s=RUN)
+            dst = target.rearrange("p (r s) t -> p r t s", s=RUN)
             if engine == "vector":
                 nc.vector.tensor_copy(out=dst, in_=src)
             elif engine == "scalar":
                 nc.scalar.copy(out=dst, in_=src)
             else:
                 nc.gpsimd.tensor_scalar(
-                    out=grouped[:],
+                    out=target,
                     in0=cols.rearrange("p t n -> p n t"),
                     scalar1=1.0,
                     scalar2=0.0,
                     op0=ALU.mult,
                     op1=ALU.add,
                 )
-            return grouped
 
         def quantise_and_project(i, c, grouped):
             b, g = divmod(i, passes)
@@ -178,10 +179,8 @@ def tile_adaattn3dstylizer_pa_t_kernel(tc, q, Wq, bq, out):
             nc.scalar.copy(out=bias[:], in_=bias_turned[:, 0:1])
         psum = ctx.enter_context(tc.psum_pool(name="psum", bufs=8))
 
-        for i in range(1, MEANS_AHEAD):
+        for i in range(1, AHEAD):
             for t in range(PACK):
-                if i == MEANS_AHEAD - 1 and t == PACK // 2:
-                    finish_statistics(0)
                 statistics_row(i, t)
         w_codes = const.tile([P, passes, P], U32, align_bytes=64)
         w_scales = const.tile([P, passes, P], U8, align_bytes=64)
@@ -191,23 +190,36 @@ def tile_adaattn3dstylizer_pa_t_kernel(tc, q, Wq, bq, out):
             in_=w_grouped[:].rearrange("p g o t -> p (g o t)"),
         )
 
+        finish_statistics(0)
         normalise(0)
 
         for i in range(tiles):
-            later = i + MEANS_AHEAD
-            grouped = {}
-            if later < tiles:
-                grouped[chunks - 1] = regroup(i, chunks - 1, "gpsimd")
-                for t in range(PACK):
-                    statistics_row(later, t)
-            if i + 1 < tiles:
-                finish_statistics(i + 1)
+            window = i + AHEAD < tiles
+            grouped = []
             for c in range(chunks):
-                if c not in grouped:
-                    grouped[c] = regroup(i, c, "scalar" if later >= tiles and c % 2 == 1 else "vector")
+                chunk_tile = group_pool.tile([P, CHUNK, PACK], BF16, align_bytes=64, name="grouped")
+                grouped.append(chunk_tile)
+            if window:
+                for first in range(positions - 3 * PIECE, positions, PIECE):
+                    regroup(i, grouped, first, PIECE, "gpsimd")
+                regroup(i, grouped, positions - 4 * PIECE, PIECE, "scalar")
+                for t in range(PACK):
+                    statistics_row(i + AHEAD, t)
+                for c in range(chunks // 2):
+                    regroup(i, grouped, c * CHUNK, CHUNK, "vector")
+            else:
+                for first in range(positions - 3 * PIECE, positions, PIECE):
+                    regroup(i, grouped, first, PIECE, "scalar")
+                for c in range(chunks // 2):
+                    regroup(i, grouped, c * CHUNK, CHUNK, "vector")
+                regroup(i, grouped, positions - 4 * PIECE, PIECE, "vector")
             if i + RAW_BUFS < tiles:
                 load(i + RAW_BUFS)
             if i + 1 < tiles:
+                finish_statistics(i + 1)
+            if i + 1 < tiles and not i + 1 + AHEAD < tiles:
                 normalise(i + 1)
             for c in range(chunks):
                 quantise_and_project(i, c, grouped[c])
+            if i + 1 + AHEAD < tiles:
+                normalise(i + 1)

@@ -12,6 +12,7 @@ U8 = mybir.dt.uint8
 FP8X4 = mybir.dt.float8_e4m3fn_x4
 ALU = mybir.AluOpType
 ACT = mybir.ActivationFunctionType
+AXIS = mybir.AxisListType
 
 EPS = 1e-5
 P = 128
@@ -23,6 +24,7 @@ RUN = 4
 PIECE = 512
 RAW_BUFS = 4
 AHEAD = 2
+FIRST_PIECES = 4
 
 
 def tile_adaattn3dstylizer_pa_t_kernel(tc, q, Wq, bq, out):
@@ -54,22 +56,36 @@ def tile_adaattn3dstylizer_pa_t_kernel(tc, q, Wq, bq, out):
             rows = q[b, g * K_PASS : (g + 1) * K_PASS, :].rearrange("(p t) n -> p t n", t=PACK)
             x[i] = raw_pool.tile([P, PACK, positions], BF16, name="x")
             for t in range(PACK):
-                nc.sync.dma_start(out=x[i][:, t, :], in_=rows[:, t, :])
+                pieces = FIRST_PIECES if i == 0 and t == 0 else 1
+                width = positions // pieces
+                for j in range(pieces):
+                    cols = slice(j * width, (j + 1) * width)
+                    nc.sync.dma_start(out=x[i][:, t, cols], in_=rows[:, t, cols])
 
         def statistics_row(i, t):
             if t == 0:
                 neg_mean[i] = stat_pool.tile([P, PACK], F32, name="neg_mean")
                 sum_sq[i] = stat_pool.tile([P, PACK], F32, name="sum_sq")
             scrap_v = scrap_pool.tile([P, positions], BF16, name="scrap_v")
-            nc.vector.tensor_scalar(
-                out=scrap_v[:],
-                in0=x[i][:, t, :],
-                scalar1=-1.0 / positions,
-                scalar2=None,
-                op0=ALU.mult,
-                op1=ALU.add,
-                accum_out=neg_mean[i][:, t : t + 1],
-            )
+            pieces = FIRST_PIECES if i == 0 and t == 0 else 1
+            width = positions // pieces
+            sums = neg_mean[i][:, t : t + 1]
+            if pieces > 1:
+                partial = const.tile([P, pieces], F32, name="partial")
+                sums = partial[:]
+            for j in range(pieces):
+                cols = slice(j * width, (j + 1) * width)
+                nc.vector.tensor_scalar(
+                    out=scrap_v[:, cols],
+                    in0=x[i][:, t, cols],
+                    scalar1=-1.0 / positions,
+                    scalar2=None,
+                    op0=ALU.mult,
+                    op1=ALU.add,
+                    accum_out=sums[:, j : j + 1],
+                )
+            if pieces > 1:
+                nc.vector.tensor_reduce(out=neg_mean[i][:, t : t + 1], in_=sums, op=ALU.add, axis=AXIS.X)
             scrap_s = scrap_pool.tile([P, positions], BF16, name="scrap_s")
             nc.scalar.activation(
                 out=scrap_s[:],
@@ -148,8 +164,9 @@ def tile_adaattn3dstylizer_pa_t_kernel(tc, q, Wq, bq, out):
                     nc.sync.dma_start(out=out[b, :, first : first + BANK], in_=result[:])
 
         w_rows = const.tile([P, channels], BF16)
-        nc.scalar.dma_start(out=w_rows[:], in_=Wq)
-        for i in range(RAW_BUFS):
+        load(0)
+        nc.sync.dma_start(out=w_rows[:], in_=Wq)
+        for i in range(1, RAW_BUFS):
             load(i)
         identity = const.tile([P, P], BF16)
         make_identity(nc, identity[:])
@@ -162,7 +179,14 @@ def tile_adaattn3dstylizer_pa_t_kernel(tc, q, Wq, bq, out):
         nc.scalar.activation(out=warm[:], in_=ones[:], func=ACT.Sqrt)
 
         w_sorted = const.tile([P, passes, PACK, P], BF16)
-        nc.vector.tensor_copy(out=w_sorted[:], in_=w_rows[:].rearrange("o (g p t) -> o g t p", g=passes, t=PACK))
+        nc.gpsimd.tensor_scalar(
+            out=w_sorted[:],
+            in0=w_rows[:].rearrange("o (g p t) -> o g t p", g=passes, t=PACK),
+            scalar1=1.0,
+            scalar2=0.0,
+            op0=ALU.mult,
+            op1=ALU.add,
+        )
 
         for t in range(PACK):
             statistics_row(0, t)

@@ -50,6 +50,7 @@ def tile_adaattn3dstylizer_pa_t_kernel(tc, q, Wq, bq, out):
         x = {}
         neg_mean, sum_sq, std, rstd = {}, {}, {}, {}
         acc = {}
+        closed = []
 
         def load(i):
             b, g = divmod(i, passes)
@@ -134,34 +135,48 @@ def tile_adaattn3dstylizer_pa_t_kernel(tc, q, Wq, bq, out):
                     op1=ALU.add,
                 )
 
-        def quantise_and_project(i, c, grouped):
+        def quantise_and_project(i, c, grouped, calls):
             b, g = divmod(i, passes)
             codes = code_pool.tile([P, CHUNK], U32, align_bytes=64, name="codes")
             scales = code_pool.tile([P, CHUNK], U8, align_bytes=64, name="scales")
-            nc.vector.quantize_mx(
-                out=codes[:].bitcast(FP8X4), scales=scales[:], in_=grouped[:].rearrange("p n t -> p (n t)")
-            )
-            for h in range(CHUNK // BANK):
-                cols = slice(h * BANK, (h + 1) * BANK)
-                if g == 0:
-                    acc[c, h] = psum.tile([P, BANK], F32, name="acc")
-                nc.tensor.matmul_mx(
-                    out=acc[c, h][:],
-                    lhsT=w_codes[:, g, :].bitcast(FP8X4),
-                    lhsT_scale=w_scales[:, g, :],
-                    rhs=codes[:, cols].bitcast(FP8X4),
-                    rhs_scale=scales[:, cols],
-                    start=(g == 0),
-                    stop=(g == passes - 1),
+            width = CHUNK // calls
+            for k in range(calls):
+                cols = slice(k * width, (k + 1) * width)
+                nc.vector.quantize_mx(
+                    out=codes[:, cols].bitcast(FP8X4),
+                    scales=scales[:, cols],
+                    in_=grouped[:, cols, :].rearrange("p n t -> p (n t)"),
                 )
-            if g == passes - 1:
-                for h in range(CHUNK // BANK):
-                    first = c * CHUNK + h * BANK
-                    result = out_pool.tile([P, BANK], F32, name="result")
+                for h in range(k * width // BANK, (k + 1) * width // BANK):
+                    cols = slice(h * BANK, (h + 1) * BANK)
+                    if g == 0:
+                        acc[c, h] = psum.tile([P, BANK], F32, name="acc")
+                    nc.tensor.matmul_mx(
+                        out=acc[c, h][:],
+                        lhsT=w_codes[:, g, :].bitcast(FP8X4),
+                        lhsT_scale=w_scales[:, g, :],
+                        rhs=codes[:, cols].bitcast(FP8X4),
+                        rhs_scale=scales[:, cols],
+                        start=(g == 0),
+                        stop=(g == passes - 1),
+                    )
+                    if g == passes - 1:
+                        closed.append((b, c, h))
+
+        def empty_banks(engines):
+            for k, (b, c, h) in enumerate(closed):
+                first = c * CHUNK + h * BANK
+                result = out_pool.tile([P, BANK], F32, name="result")
+                if engines[k % len(engines)] == "scalar":
                     nc.scalar.activation(
                         out=result[:], in_=acc[c, h][:], func=ACT.Identity, bias=bias[:, 0:1], scale=1.0
                     )
-                    nc.sync.dma_start(out=out[b, :, first : first + BANK], in_=result[:])
+                else:
+                    nc.vector.tensor_scalar(
+                        out=result[:], in0=acc[c, h][:], scalar1=bias[:, 0:1], scalar2=None, op0=ALU.add
+                    )
+                nc.sync.dma_start(out=out[b, :, first : first + BANK], in_=result[:])
+            closed.clear()
 
         w_rows = const.tile([P, channels], BF16)
         load(0)
@@ -218,32 +233,36 @@ def tile_adaattn3dstylizer_pa_t_kernel(tc, q, Wq, bq, out):
         normalise(0)
 
         for i in range(tiles):
+            last = i == tiles - 1
             window = i + AHEAD < tiles
             grouped = []
             for c in range(chunks):
                 chunk_tile = group_pool.tile([P, CHUNK, PACK], BF16, align_bytes=64, name="grouped")
                 grouped.append(chunk_tile)
+            helped = 3 if last else 4
+            scalars = 1 if window else helped
+            for k in range(scalars, helped):
+                regroup(i, grouped, positions - (helped - k) * PIECE, PIECE, "gpsimd")
+            for k in range(scalars):
+                regroup(i, grouped, positions - (helped - k) * PIECE, PIECE, "scalar")
+            empty_banks(["scalar"])
             if window:
-                for first in range(positions - 3 * PIECE, positions, PIECE):
-                    regroup(i, grouped, first, PIECE, "gpsimd")
-                regroup(i, grouped, positions - 4 * PIECE, PIECE, "scalar")
                 for t in range(PACK):
                     statistics_row(i + AHEAD, t)
-                for c in range(chunks // 2):
-                    regroup(i, grouped, c * CHUNK, CHUNK, "vector")
-            else:
-                for first in range(positions - 3 * PIECE, positions, PIECE):
-                    regroup(i, grouped, first, PIECE, "scalar")
-                for c in range(chunks // 2):
-                    regroup(i, grouped, c * CHUNK, CHUNK, "vector")
-                regroup(i, grouped, positions - 4 * PIECE, PIECE, "vector")
+            for c in range(chunks // 2):
+                regroup(i, grouped, c * CHUNK, CHUNK, "vector")
+            for first in range(chunks // 2 * CHUNK, positions - helped * PIECE, PIECE):
+                regroup(i, grouped, first, PIECE, "vector")
             if i + RAW_BUFS < tiles:
                 load(i + RAW_BUFS)
-            if i + 1 < tiles:
+            if not last:
                 finish_statistics(i + 1)
-            if i + 1 < tiles and not i + 1 + AHEAD < tiles:
+            if not last and not i + 1 + AHEAD < tiles:
                 normalise(i + 1)
             for c in range(chunks):
-                quantise_and_project(i, c, grouped[c])
+                final = last and c == chunks - 1
+                quantise_and_project(i, c, grouped[c], 2 if final else 1)
+                if last:
+                    empty_banks(["scalar", "vector"] if final else ["scalar"])
             if i + 1 + AHEAD < tiles:
                 normalise(i + 1)

@@ -239,7 +239,7 @@ def tile_adaattn3dstylizer_pa_t_kernel(tc, q, Wq, bq, out):
             for c in range(chunks):
                 chunk_tile = group_pool.tile([P, CHUNK, PACK], BF16, align_bytes=64, name="grouped")
                 grouped.append(chunk_tile)
-            helped = 3 if last else 4
+            helped = 4 if window else 3
             scalars = 1 if window else helped
             for k in range(scalars, helped):
                 regroup(i, grouped, positions - (helped - k) * PIECE, PIECE, "gpsimd")

@@ -24,6 +24,7 @@ RUN = 4
 PIECE = 512
 RAW_BUFS = 4
 AHEAD = 2
+EARLY_ROWS = 2
 FIRST_PIECES = 4
 
 
@@ -67,6 +68,8 @@ def tile_adaattn3dstylizer_pa_t_kernel(tc, q, Wq, bq, out):
             if t == 0:
                 neg_mean[i] = stat_pool.tile([P, PACK], F32, name="neg_mean")
                 sum_sq[i] = stat_pool.tile([P, PACK], F32, name="sum_sq")
+                std[i] = stat_pool.tile([P, PACK], F32, name="std")
+                rstd[i] = stat_pool.tile([P, PACK], F32, name="rstd")
             scrap_v = scrap_pool.tile([P, positions], BF16, name="scrap_v")
             pieces = FIRST_PIECES if i == 0 and t == 0 else 1
             width = positions // pieces
@@ -96,17 +99,20 @@ def tile_adaattn3dstylizer_pa_t_kernel(tc, q, Wq, bq, out):
                 scale=1.0,
                 accum_out=sum_sq[i][:, t : t + 1],
             )
-            if t == PACK - 1:
-                std[i] = stat_pool.tile([P, PACK], F32, name="std")
-                nc.scalar.activation(out=std[i][:], in_=sum_sq[i][:], func=ACT.Sqrt, bias=EPS, scale=1.0 / positions)
+            early = EARLY_ROWS if i == 0 else 0
+            if t < early or t == PACK - 1:
+                rows = slice(t, t + 1) if t < early else slice(early, PACK)
+                nc.scalar.activation(
+                    out=std[i][:, rows], in_=sum_sq[i][:, rows], func=ACT.Sqrt, bias=EPS, scale=1.0 / positions
+                )
 
-        def finish_statistics(i):
-            rstd[i] = stat_pool.tile([P, PACK], F32, name="rstd")
-            nc.vector.reciprocal(out=rstd[i][:], in_=std[i][:])
+        def finish_statistics(i, first, count):
+            rows = slice(first, first + count)
+            nc.vector.reciprocal(out=rstd[i][:, rows], in_=std[i][:, rows])
 
-        def normalise(i):
-            for t in range(PACK):
-                nc.vector.tensor_scalar(
+        def normalise(i, first, count, engine):
+            for t in range(first, first + count):
+                engine.tensor_scalar(
                     out=x[i][:, t, :],
                     in0=x[i][:, t, :],
                     scalar1=neg_mean[i][:, t : t + 1],
@@ -194,17 +200,20 @@ def tile_adaattn3dstylizer_pa_t_kernel(tc, q, Wq, bq, out):
         nc.scalar.activation(out=warm[:], in_=ones[:], func=ACT.Sqrt)
 
         w_sorted = const.tile([P, passes, PACK, P], BF16)
-        nc.gpsimd.tensor_scalar(
-            out=w_sorted[:],
-            in0=w_rows[:].rearrange("o (g p t) -> o g t p", g=passes, t=PACK),
-            scalar1=1.0,
-            scalar2=0.0,
-            op0=ALU.mult,
-            op1=ALU.add,
-        )
 
         for t in range(PACK):
             statistics_row(0, t)
+            if t == 2:
+                finish_statistics(0, 0, 1)
+                normalise(0, 0, 1, nc.gpsimd)
+                nc.gpsimd.tensor_scalar(
+                    out=w_sorted[:],
+                    in0=w_rows[:].rearrange("o (g p t) -> o g t p", g=passes, t=PACK),
+                    scalar1=1.0,
+                    scalar2=0.0,
+                    op0=ALU.mult,
+                    op1=ALU.add,
+                )
         w_grouped = const.tile([P, passes, P, PACK], BF16, align_bytes=64)
         bias = const.tile([P, 1], F32)
         with tc.psum_pool(name="setup", bufs=1) as setup:
@@ -221,6 +230,9 @@ def tile_adaattn3dstylizer_pa_t_kernel(tc, q, Wq, bq, out):
         for i in range(1, AHEAD):
             for t in range(PACK):
                 statistics_row(i, t)
+                if i == 1 and t == 0:
+                    finish_statistics(0, 1, 1)
+                    normalise(0, 1, 1, nc.gpsimd)
         w_codes = const.tile([P, passes, P], U32, align_bytes=64)
         w_scales = const.tile([P, passes, P], U8, align_bytes=64)
         nc.vector.quantize_mx(
@@ -229,8 +241,8 @@ def tile_adaattn3dstylizer_pa_t_kernel(tc, q, Wq, bq, out):
             in_=w_grouped[:].rearrange("p g o t -> p (g o t)"),
         )
 
-        finish_statistics(0)
-        normalise(0)
+        finish_statistics(0, EARLY_ROWS, PACK - EARLY_ROWS)
+        normalise(0, EARLY_ROWS, PACK - EARLY_ROWS, nc.vector)
 
         for i in range(tiles):
             last = i == tiles - 1
@@ -239,8 +251,8 @@ def tile_adaattn3dstylizer_pa_t_kernel(tc, q, Wq, bq, out):
             for c in range(chunks):
                 chunk_tile = group_pool.tile([P, CHUNK, PACK], BF16, align_bytes=64, name="grouped")
                 grouped.append(chunk_tile)
-            helped = 4 if window else 3
-            scalars = 1 if window else helped
+            helped = (3 if i == 0 else 4) if window else 3
+            scalars = helped - 3 if window else helped
             for k in range(scalars, helped):
                 regroup(i, grouped, positions - (helped - k) * PIECE, PIECE, "gpsimd")
             for k in range(scalars):
@@ -249,20 +261,21 @@ def tile_adaattn3dstylizer_pa_t_kernel(tc, q, Wq, bq, out):
             if window:
                 for t in range(PACK):
                     statistics_row(i + AHEAD, t)
-            for c in range(chunks // 2):
+            own = positions - helped * PIECE
+            for c in range(own // CHUNK):
                 regroup(i, grouped, c * CHUNK, CHUNK, "vector")
-            for first in range(chunks // 2 * CHUNK, positions - helped * PIECE, PIECE):
+            for first in range(own // CHUNK * CHUNK, own, PIECE):
                 regroup(i, grouped, first, PIECE, "vector")
             if i + RAW_BUFS < tiles:
                 load(i + RAW_BUFS)
             if not last:
-                finish_statistics(i + 1)
+                finish_statistics(i + 1, 0, PACK)
             if not last and not i + 1 + AHEAD < tiles:
-                normalise(i + 1)
+                normalise(i + 1, 0, PACK, nc.vector)
             for c in range(chunks):
                 final = last and c == chunks - 1
                 quantise_and_project(i, c, grouped[c], 2 if final else 1)
                 if last:
                     empty_banks(["scalar", "vector"] if final else ["scalar"])
             if i + 1 + AHEAD < tiles:
-                normalise(i + 1)
+                normalise(i + 1, 0, PACK, nc.vector)

@@ -255,17 +255,19 @@ def tile_adaattn3dstylizer_pa_t_kernel(tc, q, Wq, bq, out):
             scalars = helped - 3 if window else helped
             for k in range(scalars, helped):
                 regroup(i, grouped, positions - (helped - k) * PIECE, PIECE, "gpsimd")
+            if last:
+                regroup(i, grouped, positions - helped * PIECE - PIECE // 2, PIECE // 2, "scalar")
             for k in range(scalars):
                 regroup(i, grouped, positions - (helped - k) * PIECE, PIECE, "scalar")
             empty_banks(["scalar"])
             if window:
                 for t in range(PACK):
                     statistics_row(i + AHEAD, t)
-            own = positions - helped * PIECE
+            own = positions - helped * PIECE - (PIECE // 2 if last else 0)
             for c in range(own // CHUNK):
                 regroup(i, grouped, c * CHUNK, CHUNK, "vector")
-            for first in range(own // CHUNK * CHUNK, own, PIECE):
-                regroup(i, grouped, first, PIECE, "vector")
+            if own % CHUNK:
+                regroup(i, grouped, own // CHUNK * CHUNK, own % CHUNK, "vector")
             if i + RAW_BUFS < tiles:
                 load(i + RAW_BUFS)
             if not last:
@@ -274,7 +276,7 @@ def tile_adaattn3dstylizer_pa_t_kernel(tc, q, Wq, bq, out):
                 normalise(i + 1, 0, PACK, nc.vector)
             for c in range(chunks):
                 final = last and c == chunks - 1
-                quantise_and_project(i, c, grouped[c], 2 if final else 1)
+                quantise_and_project(i, c, grouped[c], 2)
                 if last:
                     empty_banks(["scalar", "vector"] if final else ["scalar"])
             if i + 1 + AHEAD < tiles:

@@ -276,7 +276,7 @@ def tile_adaattn3dstylizer_pa_t_kernel(tc, q, Wq, bq, out):
                 normalise(i + 1, 0, PACK, nc.vector)
             for c in range(chunks):
                 final = last and c == chunks - 1
-                quantise_and_project(i, c, grouped[c], 2)
+                quantise_and_project(i, c, grouped[c], 2 if final else 1)
                 if last:
                     empty_banks(["scalar", "vector"] if final else ["scalar"])
             if i + 1 + AHEAD < tiles:

@@ -23,9 +23,20 @@ CHUNK = 1024
 RUN = 4
 PIECE = 512
 RAW_BUFS = 4
-AHEAD = 2
-EARLY_ROWS = 2
+SPREAD = 8
+SHARE = 512
+GROUP = 16
+PARTS = 4
+SPREAD_BUFS = 4
+OPEN_BANKS = 7
 FIRST_PIECES = 4
+SUM_FROM = 2
+G_EARLY = 2
+S_PIECES = [0, 0, 0, 0, 0, 3]
+P_AT = [1, 1, 1, 1, 0, 0]
+K_AT = [0, 0, 2, 0, 2, 0]
+M_AT = [0, 0, 0, 0, 0, 0]
+N_AT = [2, 2, 2, 2, 2, 2]
 
 
 def tile_adaattn3dstylizer_pa_t_kernel(tc, q, Wq, bq, out):
@@ -35,22 +46,27 @@ def tile_adaattn3dstylizer_pa_t_kernel(tc, q, Wq, bq, out):
     tiles = batches * passes
     chunks = positions // CHUNK
     assert Wq.shape[0] == P and channels % K_PASS == 0 and positions % CHUNK == 0
-    assert chunks % 2 == 0 and CHUNK == 2 * PIECE
-    assert tiles >= RAW_BUFS
+    assert SPREAD * SHARE == positions and GROUP * SPREAD == P
 
     with ExitStack() as ctx:
         const = ctx.enter_context(tc.tile_pool(name="const", bufs=1))
         raw_pool = ctx.enter_context(tc.tile_pool(name="raw", bufs=RAW_BUFS))
+        spread_pool = ctx.enter_context(tc.tile_pool(name="spread", bufs=SPREAD_BUFS))
+        sum_pool = ctx.enter_context(tc.tile_pool(name="sum", bufs=1))
         stat_pool = ctx.enter_context(tc.tile_pool(name="stat", bufs=tiles))
-        scrap_pool = ctx.enter_context(tc.tile_pool(name="scrap", bufs=2))
+        scrap_pool = ctx.enter_context(tc.tile_pool(name="scrap", bufs=1))
         group_pool = ctx.enter_context(tc.tile_pool(name="group", bufs=chunks))
-        code_pool = ctx.enter_context(tc.tile_pool(name="code", bufs=3))
+        code_pool = ctx.enter_context(tc.tile_pool(name="code", bufs=2))
+        held_pool = ctx.enter_context(tc.tile_pool(name="held", bufs=1))
         out_pool = ctx.enter_context(tc.tile_pool(name="outs", bufs=8))
+        sum_psum = ctx.enter_context(tc.psum_pool(name="sums", bufs=1))
         ctx.enter_context(tc.manual_schedule())
 
         x = {}
-        neg_mean, sum_sq, std, rstd = {}, {}, {}, {}
+        neg_mean, shift, sum_sq, var, std, rstd = {}, {}, {}, {}, {}, {}
+        spread, total = {}, {}
         acc = {}
+        held = {}
         closed = []
 
         def load(i):
@@ -64,13 +80,45 @@ def tile_adaattn3dstylizer_pa_t_kernel(tc, q, Wq, bq, out):
                     cols = slice(j * width, (j + 1) * width)
                     nc.sync.dma_start(out=x[i][:, t, cols], in_=rows[:, t, cols])
 
-        def statistics_row(i, t):
-            if t == 0:
-                neg_mean[i] = stat_pool.tile([P, PACK], F32, name="neg_mean")
-                sum_sq[i] = stat_pool.tile([P, PACK], F32, name="sum_sq")
-                std[i] = stat_pool.tile([P, PACK], F32, name="std")
-                rstd[i] = stat_pool.tile([P, PACK], F32, name="rstd")
-            scrap_v = scrap_pool.tile([P, positions], BF16, name="scrap_v")
+        def load_spread(i):
+            b, g = divmod(i, passes)
+            rows = q[b, g * K_PASS : (g + 1) * K_PASS, :].rearrange("(k c) (j s) -> (c j) k s", c=GROUP, j=SPREAD)
+            groups = K_PASS // GROUP // PARTS
+            spread[i] = []
+            for part in range(PARTS):
+                piece = spread_pool.tile([P, groups, SHARE], BF16, align_bytes=64, name="spread")
+                nc.sync.dma_start(out=piece[:], in_=rows[:, part * groups : (part + 1) * groups, :])
+                spread[i].append(piece)
+
+        def sum_channels(i, part):
+            if part == 0:
+                total[i] = sum_psum.tile([P, K_PASS], F32, name="total")
+            groups = K_PASS // GROUP // PARTS
+            for k in range(groups):
+                first = (part * groups + k) * GROUP
+                for m in range(SHARE // P):
+                    nc.tensor.matmul(
+                        out=total[i][:, first : first + GROUP],
+                        lhsT=spread[i][part][:, k, m * P : (m + 1) * P],
+                        rhs=pick[:],
+                        start=(m == 0),
+                        stop=(m == SHARE // P - 1),
+                    )
+
+        def means_from_sums(i):
+            sums = sum_pool.tile([P, P, PACK], F32, align_bytes=64, name="sums")
+            nc.scalar.copy(out=sums[:].rearrange("m p t -> m (p t)"), in_=total[i][:])
+            for t in range(PACK):
+                nc.tensor.matmul(
+                    out=total[i][:, t : t + 1], lhsT=sums[:, :, t], rhs=minus_share[:], start=True, stop=True
+                )
+
+        def new_stats(i):
+            for name, store in (("neg_mean", neg_mean), ("shift", shift), ("sum_sq", sum_sq), ("var", var), ("std", std), ("rstd", rstd)):
+                store[i] = stat_pool.tile([P, PACK], F32, name=name)
+
+        def mean_row(i, t):
+            scrap_v = group_pool.tile([P, positions], BF16, align_bytes=64, name="grouped")
             pieces = FIRST_PIECES if i == 0 and t == 0 else 1
             width = positions // pieces
             sums = neg_mean[i][:, t : t + 1]
@@ -90,36 +138,58 @@ def tile_adaattn3dstylizer_pa_t_kernel(tc, q, Wq, bq, out):
                 )
             if pieces > 1:
                 nc.vector.tensor_reduce(out=neg_mean[i][:, t : t + 1], in_=sums, op=ALU.add, axis=AXIS.X)
+
+        def square_row(i, t):
+            summed = i >= SUM_FROM
             scrap_s = scrap_pool.tile([P, positions], BF16, name="scrap_s")
             nc.scalar.activation(
                 out=scrap_s[:],
                 in_=x[i][:, t, :],
                 func=ACT.Square,
-                bias=neg_mean[i][:, t : t + 1],
-                scale=1.0,
+                bias=x[i][:, t, 0:1] if summed else neg_mean[i][:, t : t + 1],
+                scale=-1.0 if summed else 1.0,
                 accum_out=sum_sq[i][:, t : t + 1],
             )
-            early = EARLY_ROWS if i == 0 else 0
-            if t < early or t == PACK - 1:
-                rows = slice(t, t + 1) if t < early else slice(early, PACK)
-                nc.scalar.activation(
-                    out=std[i][:, rows], in_=sum_sq[i][:, rows], func=ACT.Sqrt, bias=EPS, scale=1.0 / positions
-                )
 
-        def finish_statistics(i, first, count):
+        def offset(i, first, count):
+            rows = slice(first, first + count)
+            nc.vector.tensor_tensor(
+                out=shift[i][:, rows], in0=x[i][:, rows, 0], in1=neg_mean[i][:, rows], op=ALU.add
+            )
+            nc.vector.scalar_tensor_tensor(
+                out=var[i][:, rows],
+                in0=shift[i][:, rows],
+                scalar=-1.0,
+                in1=shift[i][:, rows],
+                op0=ALU.mult,
+                op1=ALU.mult,
+            )
+            nc.vector.tensor_scalar(
+                out=var[i][:, rows], in0=var[i][:, rows], scalar1=EPS, scalar2=None, op0=ALU.add
+            )
+
+        def deviation(i, t):
+            nc.scalar.activation(
+                out=std[i][:, t : t + 1],
+                in_=sum_sq[i][:, t : t + 1],
+                func=ACT.Sqrt,
+                bias=var[i][:, t : t + 1] if i >= SUM_FROM else EPS,
+                scale=1.0 / positions,
+            )
+
+        def invert(i, first, count):
             rows = slice(first, first + count)
             nc.vector.reciprocal(out=rstd[i][:, rows], in_=std[i][:, rows])
 
-        def normalise(i, first, count, engine):
-            for t in range(first, first + count):
-                engine.tensor_scalar(
-                    out=x[i][:, t, :],
-                    in0=x[i][:, t, :],
-                    scalar1=neg_mean[i][:, t : t + 1],
-                    scalar2=rstd[i][:, t : t + 1],
-                    op0=ALU.add,
-                    op1=ALU.mult,
-                )
+        def normalise(i, t, engine):
+            engine.tensor_scalar(
+                out=x[i][:, t, :],
+                in0=x[i][:, t, :],
+                scalar1=neg_mean[i][:, t : t + 1],
+                scalar2=rstd[i][:, t : t + 1],
+                op0=ALU.add,
+                op1=ALU.mult,
+            )
 
         def regroup(i, grouped, first, count, engine):
             c, start = divmod(first, CHUNK)
@@ -143,8 +213,10 @@ def tile_adaattn3dstylizer_pa_t_kernel(tc, q, Wq, bq, out):
 
         def quantise_and_project(i, c, grouped, calls):
             b, g = divmod(i, passes)
-            codes = code_pool.tile([P, CHUNK], U32, align_bytes=64, name="codes")
-            scales = code_pool.tile([P, CHUNK], U8, align_bytes=64, name="scales")
+            hold = g == 0 and (c + 1) * (CHUNK // BANK) > OPEN_BANKS
+            pool = held_pool if hold else code_pool
+            codes = pool.tile([P, CHUNK], U32, align_bytes=64, name="codes")
+            scales = pool.tile([P, CHUNK], U8, align_bytes=64, name="scales")
             width = CHUNK // calls
             for k in range(calls):
                 cols = slice(k * width, (k + 1) * width)
@@ -155,22 +227,30 @@ def tile_adaattn3dstylizer_pa_t_kernel(tc, q, Wq, bq, out):
                 )
                 for h in range(k * width // BANK, (k + 1) * width // BANK):
                     cols = slice(h * BANK, (h + 1) * BANK)
-                    if g == 0:
+                    if g == 0 and c * (CHUNK // BANK) + h >= OPEN_BANKS:
+                        held[c, h] = codes, scales
+                        continue
+                    operands = [(g, codes, scales)]
+                    if g > 0 and c * (CHUNK // BANK) + h >= OPEN_BANKS:
+                        operands = [(0,) + held[c, h]] + operands
+                    if operands[0][0] == 0:
                         acc[c, h] = psum.tile([P, BANK], F32, name="acc")
-                    nc.tensor.matmul_mx(
-                        out=acc[c, h][:],
-                        lhsT=w_codes[:, g, :].bitcast(FP8X4),
-                        lhsT_scale=w_scales[:, g, :],
-                        rhs=codes[:, cols].bitcast(FP8X4),
-                        rhs_scale=scales[:, cols],
-                        start=(g == 0),
-                        stop=(g == passes - 1),
-                    )
+                    for k_pass, pass_codes, pass_scales in operands:
+                        nc.tensor.matmul_mx(
+                            out=acc[c, h][:],
+                            lhsT=w_codes[:, k_pass, :].bitcast(FP8X4),
+                            lhsT_scale=w_scales[:, k_pass, :],
+                            rhs=pass_codes[:, cols].bitcast(FP8X4),
+                            rhs_scale=pass_scales[:, cols],
+                            start=(k_pass == 0),
+                            stop=(k_pass == passes - 1),
+                        )
                     if g == passes - 1:
                         closed.append((b, c, h))
 
-        def empty_banks(engines):
-            for k, (b, c, h) in enumerate(closed):
+        def empty_banks(engines, count=None):
+            ready = closed[:count]
+            for k, (b, c, h) in enumerate(ready):
                 first = c * CHUNK + h * BANK
                 result = out_pool.tile([P, BANK], F32, name="result")
                 if engines[k % len(engines)] == "scalar":
@@ -182,102 +262,127 @@ def tile_adaattn3dstylizer_pa_t_kernel(tc, q, Wq, bq, out):
                         out=result[:], in0=acc[c, h][:], scalar1=bias[:, 0:1], scalar2=None, op0=ALU.add
                     )
                 nc.sync.dma_start(out=out[b, :, first : first + BANK], in_=result[:])
-            closed.clear()
+            closed[:] = closed[len(ready) :]
 
-        w_rows = const.tile([P, channels], BF16)
+        w_rows = const.tile([P, channels], BF16, name="w_rows")
         load(0)
         nc.sync.dma_start(out=w_rows[:], in_=Wq)
-        for i in range(1, RAW_BUFS):
-            load(i)
-        identity = const.tile([P, P], BF16)
+        load(1)
+        identity = const.tile([P, P], BF16, name="identity")
         make_identity(nc, identity[:])
-        ones = const.tile([P, PACK], F32)
+        ones = const.tile([P, PACK], F32, name="ones")
         nc.vector.memset(ones[:], 1.0)
-        bias_rows = const.tile([P, P], BF16)
+        bias_rows = const.tile([P, P], BF16, name="bias_rows")
         nc.vector.memset(bias_rows[:], 0.0)
         nc.scalar.dma_start(out=bias_rows[0:1, :], in_=bq.rearrange("(x o) -> x o", x=1))
-        warm = const.tile([P, PACK], F32)
+        warm = const.tile([P, PACK], F32, name="warm")
         nc.scalar.activation(out=warm[:], in_=ones[:], func=ACT.Sqrt)
+        pick_sums = const.tile([P, GROUP], F32, name="pick_sums")
+        pick = const.tile([P, GROUP], BF16, name="pick")
+        nc.vector.tensor_reduce(
+            out=pick_sums[:], in_=identity[:].rearrange("p (c j) -> p c j", j=SPREAD), op=ALU.add, axis=AXIS.X
+        )
+        nc.vector.tensor_copy(out=pick[:], in_=pick_sums[:])
+        minus_share = const.tile([P, 1], F32, name="minus_share")
+        nc.vector.memset(minus_share[:], -1.0 / positions)
+        for i in range(tiles):
+            new_stats(i)
 
-        w_sorted = const.tile([P, passes, PACK, P], BF16)
+        w_grouped = sum_pool.tile([P, passes, P, PACK], BF16, align_bytes=64, name="sums")
+        load_spread(2)
+        load(2)
+        bias = const.tile([P, 1], F32, name="bias")
+        w_codes = const.tile([P, passes, P], U32, align_bytes=64, name="w_codes")
+        w_scales = const.tile([P, passes, P], U8, align_bytes=64, name="w_scales")
 
         for t in range(PACK):
-            statistics_row(0, t)
-            if t == 2:
-                finish_statistics(0, 0, 1)
-                normalise(0, 0, 1, nc.gpsimd)
-                nc.gpsimd.tensor_scalar(
-                    out=w_sorted[:],
-                    in0=w_rows[:].rearrange("o (g p t) -> o g t p", g=passes, t=PACK),
-                    scalar1=1.0,
-                    scalar2=0.0,
-                    op0=ALU.mult,
-                    op1=ALU.add,
-                )
-        w_grouped = const.tile([P, passes, P, PACK], BF16, align_bytes=64)
-        bias = const.tile([P, 1], F32)
+            mean_row(0, t)
+            square_row(0, t)
+            if t < G_EARLY:
+                deviation(0, t)
+            if 1 <= t <= G_EARLY:
+                invert(0, t - 1, 1)
+                normalise(0, t - 1, nc.gpsimd)
+        for t in range(G_EARLY, PACK):
+            deviation(0, t)
         with tc.psum_pool(name="setup", bufs=1) as setup:
-            w_turned = setup.tile([P, passes, PACK, P], BF16)
+            w_turned = setup.tile([P, passes, PACK, P], BF16, name="w_turned")
+            w_by_pass = w_rows[:].rearrange("o (g p t) -> o g p t", g=passes, t=PACK)
             for g in range(passes):
                 for t in range(PACK):
-                    nc.tensor.transpose(w_turned[:, g, t, :], w_sorted[:, g, t, :], identity[:])
-            bias_turned = setup.tile([P, P], BF16)
+                    nc.tensor.transpose(w_turned[:, g, t, :], w_by_pass[:, g, :, t], identity[:])
+            bias_turned = setup.tile([P, P], BF16, name="bias_turned")
             nc.tensor.transpose(bias_turned[:], bias_rows[:], identity[:])
             nc.scalar.copy(out=w_grouped[:], in_=w_turned[:].rearrange("p g t o -> p g o t"))
             nc.scalar.copy(out=bias[:], in_=bias_turned[:, 0:1])
-        psum = ctx.enter_context(tc.psum_pool(name="psum", bufs=8))
-
-        for i in range(1, AHEAD):
-            for t in range(PACK):
-                statistics_row(i, t)
-                if i == 1 and t == 0:
-                    finish_statistics(0, 1, 1)
-                    normalise(0, 1, 1, nc.gpsimd)
-        w_codes = const.tile([P, passes, P], U32, align_bytes=64)
-        w_scales = const.tile([P, passes, P], U8, align_bytes=64)
+        psum = ctx.enter_context(tc.psum_pool(name="psum", bufs=OPEN_BANKS))
+        mean_row(1, 0)
+        mean_row(1, 1)
+        mean_row(1, 2)
+        mean_row(1, 3)
         nc.vector.quantize_mx(
             out=w_codes[:].rearrange("p g o -> p (g o)").bitcast(FP8X4),
             scales=w_scales[:].rearrange("p g o -> p (g o)"),
             in_=w_grouped[:].rearrange("p g o t -> p (g o t)"),
         )
-
-        finish_statistics(0, EARLY_ROWS, PACK - EARLY_ROWS)
-        normalise(0, EARLY_ROWS, PACK - EARLY_ROWS, nc.vector)
-
+        invert(0, G_EARLY, PACK - G_EARLY)
+        for t in range(G_EARLY, PACK):
+            normalise(0, t, nc.vector)
         for i in range(tiles):
             last = i == tiles - 1
-            window = i + AHEAD < tiles
+            nxt = i + 1
             grouped = []
             for c in range(chunks):
                 chunk_tile = group_pool.tile([P, CHUNK, PACK], BF16, align_bytes=64, name="grouped")
                 grouped.append(chunk_tile)
-            helped = (3 if i == 0 else 4) if window else 3
-            scalars = helped - 3 if window else helped
-            for k in range(scalars, helped):
-                regroup(i, grouped, positions - (helped - k) * PIECE, PIECE, "gpsimd")
-            if last:
-                regroup(i, grouped, positions - helped * PIECE - PIECE // 2, PIECE // 2, "scalar")
-            for k in range(scalars):
-                regroup(i, grouped, positions - (helped - k) * PIECE, PIECE, "scalar")
-            empty_banks(["scalar"])
-            if window:
-                for t in range(PACK):
-                    statistics_row(i + AHEAD, t)
-            own = positions - helped * PIECE - (PIECE // 2 if last else 0)
+            helped = S_PIECES[i]
+            jobs = [("q", t) for t in range(PACK)] if not last else []
+            if not last and nxt >= SUM_FROM:
+                jobs.insert(M_AT[i], ("m", 0))
+                jobs.insert(N_AT[i], ("n", 0))
+            at = P_AT[i]
+            jobs[at:at] = [("p", k) for k in range(S_PIECES[i])]
+            if closed:
+                jobs.insert(K_AT[i], ("k", 0))
+            for what, k in jobs:
+                if what == "q":
+                    square_row(nxt, k)
+                elif what == "d":
+                    deviation(nxt, k)
+                elif what == "m":
+                    means_from_sums(nxt)
+                elif what == "n":
+                    nc.scalar.copy(out=neg_mean[nxt][:], in_=total[nxt][:, 0:PACK])
+                elif what == "p":
+                    regroup(i, grouped, positions - (helped - k) * PIECE, PIECE, "scalar")
+                else:
+                    empty_banks(["scalar"])
+            own = positions - helped * PIECE
             for c in range(own // CHUNK):
                 regroup(i, grouped, c * CHUNK, CHUNK, "vector")
             if own % CHUNK:
                 regroup(i, grouped, own // CHUNK * CHUNK, own % CHUNK, "vector")
-            if i + RAW_BUFS < tiles:
-                load(i + RAW_BUFS)
-            if not last:
-                finish_statistics(i + 1, 0, PACK)
-            if not last and not i + 1 + AHEAD < tiles:
-                normalise(i + 1, 0, PACK, nc.vector)
+            if SUM_FROM <= i + 2 < tiles:
+                for part in range(PARTS):
+                    sum_channels(i + 2, part)
+            if i + 3 < tiles:
+                load_spread(i + 3)
+                load(i + 3)
+            if SUM_FROM <= nxt < tiles:
+                offset(nxt, 0, PACK)
+                for t in range(PACK):
+                    deviation(nxt, t)
+            elif not last:
+                for t in range(PACK):
+                    deviation(nxt, t)
             for c in range(chunks):
                 final = last and c == chunks - 1
                 quantise_and_project(i, c, grouped[c], 2 if final else 1)
                 if last:
                     empty_banks(["scalar", "vector"] if final else ["scalar"])
-            if i + 1 + AHEAD < tiles:
-                normalise(i + 1, 0, PACK, nc.vector)
+                elif c == chunks - 2:
+                    empty_banks(["vector"], 1)
+            if not last:
+                invert(nxt, 0, PACK)
+                for t in range(PACK):
+                    normalise(nxt, t, nc.vector)

@@ -153,19 +153,14 @@ def tile_adaattn3dstylizer_pa_t_kernel(tc, q, Wq, bq, out):
 
         def offset(i, first, count):
             rows = slice(first, first + count)
-            nc.vector.tensor_tensor(
+            nc.gpsimd.tensor_tensor(
                 out=shift[i][:, rows], in0=x[i][:, rows, 0], in1=neg_mean[i][:, rows], op=ALU.add
             )
-            nc.vector.scalar_tensor_tensor(
-                out=var[i][:, rows],
-                in0=shift[i][:, rows],
-                scalar=-1.0,
-                in1=shift[i][:, rows],
-                op0=ALU.mult,
-                op1=ALU.mult,
+            nc.gpsimd.tensor_tensor(
+                out=var[i][:, rows], in0=shift[i][:, rows], in1=shift[i][:, rows], op=ALU.mult
             )
-            nc.vector.tensor_scalar(
-                out=var[i][:, rows], in0=var[i][:, rows], scalar1=EPS, scalar2=None, op0=ALU.add
+            nc.gpsimd.tensor_scalar(
+                out=var[i][:, rows], in0=var[i][:, rows], scalar1=-1.0, scalar2=EPS, op0=ALU.mult, op1=ALU.add
             )
 
         def deviation(i, t):

@@ -31,8 +31,7 @@ SPREAD_BUFS = 4
 OPEN_BANKS = 7
 FIRST_PIECES = 4
 SUM_FROM = 2
-G_EARLY = 2
-S_PIECES = [0, 0, 0, 0, 0, 3]
+S_PIECES = [0, 0, 0, 0, 0, 4]
 P_AT = [1, 1, 1, 1, 0, 0]
 K_AT = [0, 0, 2, 0, 2, 0]
 M_AT = [0, 0, 0, 0, 0, 0]
@@ -140,16 +139,29 @@ def tile_adaattn3dstylizer_pa_t_kernel(tc, q, Wq, bq, out):
                 nc.vector.tensor_reduce(out=neg_mean[i][:, t : t + 1], in_=sums, op=ALU.add, axis=AXIS.X)
 
         def square_row(i, t):
-            summed = i >= SUM_FROM
+            shifted = i != 1
             scrap_s = scrap_pool.tile([P, positions], BF16, name="scrap_s")
-            nc.scalar.activation(
-                out=scrap_s[:],
-                in_=x[i][:, t, :],
-                func=ACT.Square,
-                bias=x[i][:, t, 0:1] if summed else neg_mean[i][:, t : t + 1],
-                scale=-1.0 if summed else 1.0,
-                accum_out=sum_sq[i][:, t : t + 1],
-            )
+            pieces = FIRST_PIECES if i == 0 and t == 0 else 1
+            width = positions // pieces
+            sums = sum_sq[i][:, t : t + 1]
+            if pieces > 1:
+                partial_sq = const.tile([P, pieces], F32, name="partial_sq")
+                sums = partial_sq[:]
+            for j in range(pieces):
+                cols = slice(j * width, (j + 1) * width)
+                nc.scalar.activation(
+                    out=scrap_s[:, cols],
+                    in_=x[i][:, t, cols],
+                    func=ACT.Square,
+                    bias=x[i][:, t, 0:1] if shifted else neg_mean[i][:, t : t + 1],
+                    scale=-1.0 if shifted else 1.0,
+                    accum_out=sums[:, j : j + 1],
+                )
+            if pieces > 1:
+                unused = const.tile([P, pieces], F32, name="unused")
+                nc.scalar.activation(
+                    out=unused[:], in_=sums, func=ACT.Identity, accum_out=sum_sq[i][:, t : t + 1]
+                )
 
         def offset(i, first, count):
             rows = slice(first, first + count)
@@ -168,7 +180,7 @@ def tile_adaattn3dstylizer_pa_t_kernel(tc, q, Wq, bq, out):
                 out=std[i][:, t : t + 1],
                 in_=sum_sq[i][:, t : t + 1],
                 func=ACT.Sqrt,
-                bias=var[i][:, t : t + 1] if i >= SUM_FROM else EPS,
+                bias=var[i][:, t : t + 1] if i != 1 else EPS,
                 scale=1.0 / positions,
             )
 
@@ -176,10 +188,10 @@ def tile_adaattn3dstylizer_pa_t_kernel(tc, q, Wq, bq, out):
             rows = slice(first, first + count)
             nc.vector.reciprocal(out=rstd[i][:, rows], in_=std[i][:, rows])
 
-        def normalise(i, t, engine):
+        def normalise(i, t, engine, cols=slice(0, positions)):
             engine.tensor_scalar(
-                out=x[i][:, t, :],
-                in0=x[i][:, t, :],
+                out=x[i][:, t, cols],
+                in0=x[i][:, t, cols],
                 scalar1=neg_mean[i][:, t : t + 1],
                 scalar2=rstd[i][:, t : t + 1],
                 op0=ALU.add,
@@ -290,16 +302,26 @@ def tile_adaattn3dstylizer_pa_t_kernel(tc, q, Wq, bq, out):
         w_codes = const.tile([P, passes, P], U32, align_bytes=64, name="w_codes")
         w_scales = const.tile([P, passes, P], U8, align_bytes=64, name="w_scales")
 
-        for t in range(PACK):
-            mean_row(0, t)
-            square_row(0, t)
-            if t < G_EARLY:
-                deviation(0, t)
-            if 1 <= t <= G_EARLY:
-                invert(0, t - 1, 1)
-                normalise(0, t - 1, nc.gpsimd)
-        for t in range(G_EARLY, PACK):
-            deviation(0, t)
+        mean_row(0, 0)
+        square_row(0, 0)
+        mean_row(0, 1)
+        square_row(0, 1)
+        offset(0, 0, 1)
+        deviation(0, 0)
+        mean_row(0, 2)
+        square_row(0, 2)
+        offset(0, 1, 1)
+        deviation(0, 1)
+        invert(0, 0, 1)
+        normalise(0, 0, nc.gpsimd)
+        mean_row(0, 3)
+        square_row(0, 3)
+        offset(0, 2, 2)
+        deviation(0, 2)
+        deviation(0, 3)
+        mean_row(1, 0)
+        invert(0, 1, 1)
+        normalise(0, 1, nc.gpsimd)
         with tc.psum_pool(name="setup", bufs=1) as setup:
             w_turned = setup.tile([P, passes, PACK, P], BF16, name="w_turned")
             w_by_pass = w_rows[:].rearrange("o (g p t) -> o g p t", g=passes, t=PACK)
@@ -311,7 +333,6 @@ def tile_adaattn3dstylizer_pa_t_kernel(tc, q, Wq, bq, out):
             nc.scalar.copy(out=w_grouped[:], in_=w_turned[:].rearrange("p g t o -> p g o t"))
             nc.scalar.copy(out=bias[:], in_=bias_turned[:, 0:1])
         psum = ctx.enter_context(tc.psum_pool(name="psum", bufs=OPEN_BANKS))
-        mean_row(1, 0)
         mean_row(1, 1)
         mean_row(1, 2)
         mean_row(1, 3)
@@ -320,8 +341,8 @@ def tile_adaattn3dstylizer_pa_t_kernel(tc, q, Wq, bq, out):
             scales=w_scales[:].rearrange("p g o -> p (g o)"),
             in_=w_grouped[:].rearrange("p g o t -> p (g o t)"),
         )
-        invert(0, G_EARLY, PACK - G_EARLY)
-        for t in range(G_EARLY, PACK):
+        invert(0, 2, 2)
+        for t in range(2, PACK):
             normalise(0, t, nc.vector)
         for i in range(tiles):
             last = i == tiles - 1
@@ -379,5 +400,8 @@ def tile_adaattn3dstylizer_pa_t_kernel(tc, q, Wq, bq, out):
                     empty_banks(["vector"], 1)
             if not last:
                 invert(nxt, 0, PACK)
-                for t in range(PACK):
-                    normalise(nxt, t, nc.vector)
+                halves = 2 if nxt == tiles - 1 else 1
+                for part in reversed(range(halves)):
+                    width = positions // halves
+                    for t in range(PACK):
+                        normalise(nxt, t, nc.vector, slice(part * width, (part + 1) * width))

@@ -31,6 +31,8 @@ SPREAD_BUFS = 4
 OPEN_BANKS = 7
 FIRST_PIECES = 4
 SUM_FROM = 2
+V_BANKS = 2
+G_TAKE = 0
 S_PIECES = [0, 0, 0, 0, 0, 4]
 P_AT = [1, 1, 1, 1, 0, 0]
 K_AT = [0, 0, 2, 0, 2, 0]
@@ -352,6 +354,12 @@ def tile_adaattn3dstylizer_pa_t_kernel(tc, q, Wq, bq, out):
                 chunk_tile = group_pool.tile([P, CHUNK, PACK], BF16, align_bytes=64, name="grouped")
                 grouped.append(chunk_tile)
             helped = S_PIECES[i]
+            taken = helped * PIECE
+            if closed and not last:
+                if G_TAKE:
+                    taken += G_TAKE
+                    regroup(i, grouped, positions - G_TAKE, G_TAKE, "gpsimd")
+                empty_banks(["vector"], V_BANKS)
             jobs = [("q", t) for t in range(PACK)] if not last else []
             if not last and nxt >= SUM_FROM:
                 jobs.insert(M_AT[i], ("m", 0))
@@ -373,7 +381,7 @@ def tile_adaattn3dstylizer_pa_t_kernel(tc, q, Wq, bq, out):
                     regroup(i, grouped, positions - (helped - k) * PIECE, PIECE, "scalar")
                 else:
                     empty_banks(["scalar"])
-            own = positions - helped * PIECE
+            own = positions - taken
             for c in range(own // CHUNK):
                 regroup(i, grouped, c * CHUNK, CHUNK, "vector")
             if own % CHUNK:

@@ -31,11 +31,12 @@ SPREAD_BUFS = 4
 OPEN_BANKS = 7
 FIRST_PIECES = 4
 SUM_FROM = 2
+SHIFTED = [2, 0, 1, 1, 1, 1]
 V_BANKS = 2
 G_TAKE = 0
 S_PIECES = [0, 0, 0, 0, 0, 4]
 P_AT = [1, 1, 1, 1, 0, 0]
-K_AT = [0, 0, 2, 0, 2, 0]
+K_AT = [0, 0, 3, 0, 3, 0]
 M_AT = [0, 0, 0, 0, 0, 0]
 N_AT = [2, 2, 2, 2, 2, 2]
 
@@ -141,7 +142,7 @@ def tile_adaattn3dstylizer_pa_t_kernel(tc, q, Wq, bq, out):
                 nc.vector.tensor_reduce(out=neg_mean[i][:, t : t + 1], in_=sums, op=ALU.add, axis=AXIS.X)
 
         def square_row(i, t):
-            shifted = i != 1
+            shifted = t < SHIFTED[i]
             scrap_s = scrap_pool.tile([P, positions], BF16, name="scrap_s")
             pieces = FIRST_PIECES if i == 0 and t == 0 else 1
             width = positions // pieces
@@ -177,12 +178,13 @@ def tile_adaattn3dstylizer_pa_t_kernel(tc, q, Wq, bq, out):
                 out=var[i][:, rows], in0=var[i][:, rows], scalar1=-1.0, scalar2=EPS, op0=ALU.mult, op1=ALU.add
             )
 
-        def deviation(i, t):
+        def deviation(i, first, count):
+            rows = slice(first, first + count)
             nc.scalar.activation(
-                out=std[i][:, t : t + 1],
-                in_=sum_sq[i][:, t : t + 1],
+                out=std[i][:, rows],
+                in_=sum_sq[i][:, rows],
                 func=ACT.Sqrt,
-                bias=var[i][:, t : t + 1] if i != 1 else EPS,
+                bias=var[i][:, rows] if first < SHIFTED[i] else EPS,
                 scale=1.0 / positions,
             )
 
@@ -309,18 +311,16 @@ def tile_adaattn3dstylizer_pa_t_kernel(tc, q, Wq, bq, out):
         mean_row(0, 1)
         square_row(0, 1)
         offset(0, 0, 1)
-        deviation(0, 0)
+        deviation(0, 0, 1)
         mean_row(0, 2)
         square_row(0, 2)
         offset(0, 1, 1)
-        deviation(0, 1)
+        deviation(0, 1, 1)
         invert(0, 0, 1)
         normalise(0, 0, nc.gpsimd)
         mean_row(0, 3)
         square_row(0, 3)
-        offset(0, 2, 2)
-        deviation(0, 2)
-        deviation(0, 3)
+        deviation(0, 2, 2)
         mean_row(1, 0)
         invert(0, 1, 1)
         normalise(0, 1, nc.gpsimd)
@@ -371,8 +371,6 @@ def tile_adaattn3dstylizer_pa_t_kernel(tc, q, Wq, bq, out):
             for what, k in jobs:
                 if what == "q":
                     square_row(nxt, k)
-                elif what == "d":
-                    deviation(nxt, k)
                 elif what == "m":
                     means_from_sums(nxt)
                 elif what == "n":
@@ -392,18 +390,16 @@ def tile_adaattn3dstylizer_pa_t_kernel(tc, q, Wq, bq, out):
             if i + 3 < tiles:
                 load_spread(i + 3)
                 load(i + 3)
-            if SUM_FROM <= nxt < tiles:
-                offset(nxt, 0, PACK)
-                for t in range(PACK):
-                    deviation(nxt, t)
-            elif not last:
-                for t in range(PACK):
-                    deviation(nxt, t)
+            if not last:
+                if SHIFTED[nxt]:
+                    offset(nxt, 0, SHIFTED[nxt])
+                    deviation(nxt, 0, SHIFTED[nxt])
+                deviation(nxt, SHIFTED[nxt], PACK - SHIFTED[nxt])
             for c in range(chunks):
                 final = last and c == chunks - 1
                 quantise_and_project(i, c, grouped[c], 2 if final else 1)
                 if last:
-                    empty_banks(["scalar", "vector"] if final else ["scalar"])
+                    empty_banks(["vector"] if final else ["scalar"])
                 elif c == chunks - 2:
                     empty_banks(["vector"], 1)
             if not last:

from contextlib import ExitStack

import concourse.mybir as mybir
from concourse.masks import make_identity

FLOPS = 2 * 3 * 128 * 1024 * 4096

F32 = mybir.dt.float32
BF16 = mybir.dt.bfloat16
U32 = mybir.dt.uint32
U8 = mybir.dt.uint8
FP8X4 = mybir.dt.float8_e4m3fn_x4
ALU = mybir.AluOpType
ACT = mybir.ActivationFunctionType
AXIS = mybir.AxisListType

EPS = 1e-5
P = 128
PACK = 4
K_PASS = P * PACK
BANK = 512
CHUNK = 1024
RUN = 4
PIECE = 512
RAW_BUFS = 4
SPREAD = 8
SHARE = 512
GROUP = 16
PARTS = 4
SPREAD_BUFS = 4
OPEN_BANKS = 7
FIRST_PIECES = 4
SUM_FROM = 2
SHIFTED = [2, 0, 1, 1, 1, 1]
V_BANKS = 2
G_TAKE = 0
S_PIECES = [0, 0, 0, 0, 0, 4]
P_AT = [1, 1, 1, 1, 0, 0]
K_AT = [0, 0, 3, 0, 3, 0]
M_AT = [0, 0, 0, 0, 0, 0]
N_AT = [2, 2, 2, 2, 2, 2]


def tile_adaattn3dstylizer_pa_t_kernel(tc, q, Wq, bq, out):
    nc = tc.nc
    batches, channels, positions = q.shape
    passes = channels // K_PASS
    tiles = batches * passes
    chunks = positions // CHUNK
    assert Wq.shape[0] == P and channels % K_PASS == 0 and positions % CHUNK == 0
    assert SPREAD * SHARE == positions and GROUP * SPREAD == P

    with ExitStack() as ctx:
        const = ctx.enter_context(tc.tile_pool(name="const", bufs=1))
        raw_pool = ctx.enter_context(tc.tile_pool(name="raw", bufs=RAW_BUFS))
        spread_pool = ctx.enter_context(tc.tile_pool(name="spread", bufs=SPREAD_BUFS))
        sum_pool = ctx.enter_context(tc.tile_pool(name="sum", bufs=1))
        stat_pool = ctx.enter_context(tc.tile_pool(name="stat", bufs=tiles))
        scrap_pool = ctx.enter_context(tc.tile_pool(name="scrap", bufs=1))
        group_pool = ctx.enter_context(tc.tile_pool(name="group", bufs=chunks))
        code_pool = ctx.enter_context(tc.tile_pool(name="code", bufs=2))
        held_pool = ctx.enter_context(tc.tile_pool(name="held", bufs=1))
        out_pool = ctx.enter_context(tc.tile_pool(name="outs", bufs=8))
        sum_psum = ctx.enter_context(tc.psum_pool(name="sums", bufs=1))
        ctx.enter_context(tc.manual_schedule())

        x = {}
        neg_mean, shift, sum_sq, var, std, rstd = {}, {}, {}, {}, {}, {}
        spread, total = {}, {}
        acc = {}
        held = {}
        closed = []

        def load(i):
            b, g = divmod(i, passes)
            rows = q[b, g * K_PASS : (g + 1) * K_PASS, :].rearrange("(p t) n -> p t n", t=PACK)
            x[i] = raw_pool.tile([P, PACK, positions], BF16, name="x")
            for t in range(PACK):
                pieces = FIRST_PIECES if i == 0 and t == 0 else 1
                width = positions // pieces
                for j in range(pieces):
                    cols = slice(j * width, (j + 1) * width)
                    nc.sync.dma_start(out=x[i][:, t, cols], in_=rows[:, t, cols])

        def load_spread(i):
            b, g = divmod(i, passes)
            rows = q[b, g * K_PASS : (g + 1) * K_PASS, :].rearrange("(k c) (j s) -> (c j) k s", c=GROUP, j=SPREAD)
            groups = K_PASS // GROUP // PARTS
            spread[i] = []
            for part in range(PARTS):
                piece = spread_pool.tile([P, groups, SHARE], BF16, align_bytes=64, name="spread")
                nc.sync.dma_start(out=piece[:], in_=rows[:, part * groups : (part + 1) * groups, :])
                spread[i].append(piece)

        def sum_channels(i, part):
            if part == 0:
                total[i] = sum_psum.tile([P, K_PASS], F32, name="total")
            groups = K_PASS // GROUP // PARTS
            for k in range(groups):
                first = (part * groups + k) * GROUP
                for m in range(SHARE // P):
                    nc.tensor.matmul(
                        out=total[i][:, first : first + GROUP],
                        lhsT=spread[i][part][:, k, m * P : (m + 1) * P],
                        rhs=pick[:],
                        start=(m == 0),
                        stop=(m == SHARE // P - 1),
                    )

        def means_from_sums(i):
            sums = sum_pool.tile([P, P, PACK], F32, align_bytes=64, name="sums")
            nc.scalar.copy(out=sums[:].rearrange("m p t -> m (p t)"), in_=total[i][:])
            for t in range(PACK):
                nc.tensor.matmul(
                    out=total[i][:, t : t + 1], lhsT=sums[:, :, t], rhs=minus_share[:], start=True, stop=True
                )

        def new_stats(i):
            for name, store in (("neg_mean", neg_mean), ("shift", shift), ("sum_sq", sum_sq), ("var", var), ("std", std), ("rstd", rstd)):
                store[i] = stat_pool.tile([P, PACK], F32, name=name)

        def mean_row(i, t):
            scrap_v = group_pool.tile([P, positions], BF16, align_bytes=64, name="grouped")
            pieces = FIRST_PIECES if i == 0 and t == 0 else 1
            width = positions // pieces
            sums = neg_mean[i][:, t : t + 1]
            if pieces > 1:
                partial = const.tile([P, pieces], F32, name="partial")
                sums = partial[:]
            for j in range(pieces):
                cols = slice(j * width, (j + 1) * width)
                nc.vector.tensor_scalar(
                    out=scrap_v[:, cols],
                    in0=x[i][:, t, cols],
                    scalar1=-1.0 / positions,
                    scalar2=None,
                    op0=ALU.mult,
                    op1=ALU.add,
                    accum_out=sums[:, j : j + 1],
                )
            if pieces > 1:
                nc.vector.tensor_reduce(out=neg_mean[i][:, t : t + 1], in_=sums, op=ALU.add, axis=AXIS.X)

        def square_row(i, t):
            shifted = t < SHIFTED[i]
            scrap_s = scrap_pool.tile([P, positions], BF16, name="scrap_s")
            pieces = FIRST_PIECES if i == 0 and t == 0 else 1
            width = positions // pieces
            sums = sum_sq[i][:, t : t + 1]
            if pieces > 1:
                partial_sq = const.tile([P, pieces], F32, name="partial_sq")
                sums = partial_sq[:]
            for j in range(pieces):
                cols = slice(j * width, (j + 1) * width)
                nc.scalar.activation(
                    out=scrap_s[:, cols],
                    in_=x[i][:, t, cols],
                    func=ACT.Square,
                    bias=x[i][:, t, 0:1] if shifted else neg_mean[i][:, t : t + 1],
                    scale=-1.0 if shifted else 1.0,
                    accum_out=sums[:, j : j + 1],
                )
            if pieces > 1:
                unused = const.tile([P, pieces], F32, name="unused")
                nc.scalar.activation(
                    out=unused[:], in_=sums, func=ACT.Identity, accum_out=sum_sq[i][:, t : t + 1]
                )

        def offset(i, first, count):
            rows = slice(first, first + count)
            nc.gpsimd.tensor_tensor(
                out=shift[i][:, rows], in0=x[i][:, rows, 0], in1=neg_mean[i][:, rows], op=ALU.add
            )
            nc.gpsimd.tensor_tensor(
                out=var[i][:, rows], in0=shift[i][:, rows], in1=shift[i][:, rows], op=ALU.mult
            )
            nc.gpsimd.tensor_scalar(
                out=var[i][:, rows], in0=var[i][:, rows], scalar1=-1.0, scalar2=EPS, op0=ALU.mult, op1=ALU.add
            )

        def deviation(i, first, count):
            rows = slice(first, first + count)
            nc.scalar.activation(
                out=std[i][:, rows],
                in_=sum_sq[i][:, rows],
                func=ACT.Sqrt,
                bias=var[i][:, rows] if first < SHIFTED[i] else EPS,
                scale=1.0 / positions,
            )

        def invert(i, first, count):
            rows = slice(first, first + count)
            nc.vector.reciprocal(out=rstd[i][:, rows], in_=std[i][:, rows])

        def normalise(i, t, engine, cols=slice(0, positions)):
            engine.tensor_scalar(
                out=x[i][:, t, cols],
                in0=x[i][:, t, cols],
                scalar1=neg_mean[i][:, t : t + 1],
                scalar2=rstd[i][:, t : t + 1],
                op0=ALU.add,
                op1=ALU.mult,
            )

        def regroup(i, grouped, first, count, engine):
            c, start = divmod(first, CHUNK)
            target = grouped[c][:, start : start + count, :]
            cols = x[i][:, :, first : first + count]
            src = cols.rearrange("p t (r s) -> p r t s", s=RUN)
            dst = target.rearrange("p (r s) t -> p r t s", s=RUN)
            if engine == "vector":
                nc.vector.tensor_copy(out=dst, in_=src)
            elif engine == "scalar":
                nc.scalar.copy(out=dst, in_=src)
            else:
                nc.gpsimd.tensor_scalar(
                    out=target,
                    in0=cols.rearrange("p t n -> p n t"),
                    scalar1=1.0,
                    scalar2=0.0,
                    op0=ALU.mult,
                    op1=ALU.add,
                )

        def quantise_and_project(i, c, grouped, calls):
            b, g = divmod(i, passes)
            hold = g == 0 and (c + 1) * (CHUNK // BANK) > OPEN_BANKS
            pool = held_pool if hold else code_pool
            codes = pool.tile([P, CHUNK], U32, align_bytes=64, name="codes")
            scales = pool.tile([P, CHUNK], U8, align_bytes=64, name="scales")
            width = CHUNK // calls
            for k in range(calls):
                cols = slice(k * width, (k + 1) * width)
                nc.vector.quantize_mx(
                    out=codes[:, cols].bitcast(FP8X4),
                    scales=scales[:, cols],
                    in_=grouped[:, cols, :].rearrange("p n t -> p (n t)"),
                )
                for h in range(k * width // BANK, (k + 1) * width // BANK):
                    cols = slice(h * BANK, (h + 1) * BANK)
                    if g == 0 and c * (CHUNK // BANK) + h >= OPEN_BANKS:
                        held[c, h] = codes, scales
                        continue
                    operands = [(g, codes, scales)]
                    if g > 0 and c * (CHUNK // BANK) + h >= OPEN_BANKS:
                        operands = [(0,) + held[c, h]] + operands
                    if operands[0][0] == 0:
                        acc[c, h] = psum.tile([P, BANK], F32, name="acc")
                    for k_pass, pass_codes, pass_scales in operands:
                        nc.tensor.matmul_mx(
                            out=acc[c, h][:],
                            lhsT=w_codes[:, k_pass, :].bitcast(FP8X4),
                            lhsT_scale=w_scales[:, k_pass, :],
                            rhs=pass_codes[:, cols].bitcast(FP8X4),
                            rhs_scale=pass_scales[:, cols],
                            start=(k_pass == 0),
                            stop=(k_pass == passes - 1),
                        )
                    if g == passes - 1:
                        closed.append((b, c, h))

        def empty_banks(engines, count=None):
            ready = closed[:count]
            for k, (b, c, h) in enumerate(ready):
                first = c * CHUNK + h * BANK
                result = out_pool.tile([P, BANK], F32, name="result")
                if engines[k % len(engines)] == "scalar":
                    nc.scalar.activation(
                        out=result[:], in_=acc[c, h][:], func=ACT.Identity, bias=bias[:, 0:1], scale=1.0
                    )
                else:
                    nc.vector.tensor_scalar(
                        out=result[:], in0=acc[c, h][:], scalar1=bias[:, 0:1], scalar2=None, op0=ALU.add
                    )
                nc.sync.dma_start(out=out[b, :, first : first + BANK], in_=result[:])
            closed[:] = closed[len(ready) :]

        w_rows = const.tile([P, channels], BF16, name="w_rows")
        load(0)
        nc.sync.dma_start(out=w_rows[:], in_=Wq)
        load(1)
        identity = const.tile([P, P], BF16, name="identity")
        make_identity(nc, identity[:])
        ones = const.tile([P, PACK], F32, name="ones")
        nc.vector.memset(ones[:], 1.0)
        bias_rows = const.tile([P, P], BF16, name="bias_rows")
        nc.vector.memset(bias_rows[:], 0.0)
        nc.scalar.dma_start(out=bias_rows[0:1, :], in_=bq.rearrange("(x o) -> x o", x=1))
        warm = const.tile([P, PACK], F32, name="warm")
        nc.scalar.activation(out=warm[:], in_=ones[:], func=ACT.Sqrt)
        pick_sums = const.tile([P, GROUP], F32, name="pick_sums")
        pick = const.tile([P, GROUP], BF16, name="pick")
        nc.vector.tensor_reduce(
            out=pick_sums[:], in_=identity[:].rearrange("p (c j) -> p c j", j=SPREAD), op=ALU.add, axis=AXIS.X
        )
        nc.vector.tensor_copy(out=pick[:], in_=pick_sums[:])
        minus_share = const.tile([P, 1], F32, name="minus_share")
        nc.vector.memset(minus_share[:], -1.0 / positions)
        for i in range(tiles):
            new_stats(i)

        w_grouped = sum_pool.tile([P, passes, P, PACK], BF16, align_bytes=64, name="sums")
        load_spread(2)
        load(2)
        bias = const.tile([P, 1], F32, name="bias")
        w_codes = const.tile([P, passes, P], U32, align_bytes=64, name="w_codes")
        w_scales = const.tile([P, passes, P], U8, align_bytes=64, name="w_scales")

        mean_row(0, 0)
        square_row(0, 0)
        mean_row(0, 1)
        square_row(0, 1)
        offset(0, 0, 1)
        deviation(0, 0, 1)
        mean_row(0, 2)
        square_row(0, 2)
        offset(0, 1, 1)
        deviation(0, 1, 1)
        invert(0, 0, 1)
        normalise(0, 0, nc.gpsimd)
        mean_row(0, 3)
        square_row(0, 3)
        deviation(0, 2, 2)
        mean_row(1, 0)
        invert(0, 1, 1)
        normalise(0, 1, nc.gpsimd)
        with tc.psum_pool(name="setup", bufs=1) as setup:
            w_turned = setup.tile([P, passes, PACK, P], BF16, name="w_turned")
            w_by_pass = w_rows[:].rearrange("o (g p t) -> o g p t", g=passes, t=PACK)
            for g in range(passes):
                for t in range(PACK):
                    nc.tensor.transpose(w_turned[:, g, t, :], w_by_pass[:, g, :, t], identity[:])
            bias_turned = setup.tile([P, P], BF16, name="bias_turned")
            nc.tensor.transpose(bias_turned[:], bias_rows[:], identity[:])
            nc.scalar.copy(out=w_grouped[:], in_=w_turned[:].rearrange("p g t o -> p g o t"))
            nc.scalar.copy(out=bias[:], in_=bias_turned[:, 0:1])
        psum = ctx.enter_context(tc.psum_pool(name="psum", bufs=OPEN_BANKS))
        mean_row(1, 1)
        mean_row(1, 2)
        mean_row(1, 3)
        nc.vector.quantize_mx(
            out=w_codes[:].rearrange("p g o -> p (g o)").bitcast(FP8X4),
            scales=w_scales[:].rearrange("p g o -> p (g o)"),
            in_=w_grouped[:].rearrange("p g o t -> p (g o t)"),
        )
        invert(0, 2, 2)
        for t in range(2, PACK):
            normalise(0, t, nc.vector)
        for i in range(tiles):
            last = i == tiles - 1
            nxt = i + 1
            grouped = []
            for c in range(chunks):
                chunk_tile = group_pool.tile([P, CHUNK, PACK], BF16, align_bytes=64, name="grouped")
                grouped.append(chunk_tile)
            helped = S_PIECES[i]
            taken = helped * PIECE
            if closed and not last:
                if G_TAKE:
                    taken += G_TAKE
                    regroup(i, grouped, positions - G_TAKE, G_TAKE, "gpsimd")
                empty_banks(["vector"], V_BANKS)
            jobs = [("q", t) for t in range(PACK)] if not last else []
            if not last and nxt >= SUM_FROM:
                jobs.insert(M_AT[i], ("m", 0))
                jobs.insert(N_AT[i], ("n", 0))
            at = P_AT[i]
            jobs[at:at] = [("p", k) for k in range(S_PIECES[i])]
            if closed:
                jobs.insert(K_AT[i], ("k", 0))
            for what, k in jobs:
                if what == "q":
                    square_row(nxt, k)
                elif what == "m":
                    means_from_sums(nxt)
                elif what == "n":
                    nc.scalar.copy(out=neg_mean[nxt][:], in_=total[nxt][:, 0:PACK])
                elif what == "p":
                    regroup(i, grouped, positions - (helped - k) * PIECE, PIECE, "scalar")
                else:
                    empty_banks(["scalar"])
            own = positions - taken
            for c in range(own // CHUNK):
                regroup(i, grouped, c * CHUNK, CHUNK, "vector")
            if own % CHUNK:
                regroup(i, grouped, own // CHUNK * CHUNK, own % CHUNK, "vector")
            if SUM_FROM <= i + 2 < tiles:
                for part in range(PARTS):
                    sum_channels(i + 2, part)
            if i + 3 < tiles:
                load_spread(i + 3)
                load(i + 3)
            if not last:
                if SHIFTED[nxt]:
                    offset(nxt, 0, SHIFTED[nxt])
                    deviation(nxt, 0, SHIFTED[nxt])
                deviation(nxt, SHIFTED[nxt], PACK - SHIFTED[nxt])
            for c in range(chunks):
                final = last and c == chunks - 1
                quantise_and_project(i, c, grouped[c], 2 if final else 1)
                if last:
                    empty_banks(["vector"] if final else ["scalar"])
                elif c == chunks - 2:
                    empty_banks(["vector"], 1)
            if not last:
                invert(nxt, 0, PACK)
                halves = 2 if nxt == tiles - 1 else 1
                for part in reversed(range(halves)):
                    width = positions // halves
                    for t in range(PACK):
                        normalise(nxt, t, nc.vector, slice(part * width, (part + 1) * width))
